import numpy as np
import ml_dtypes


def mxq(x, axis, fmt="e4m3"):
    dtype, down = {"e4m3": (ml_dtypes.float8_e4m3fn, 7), "e5m2": (ml_dtypes.float8_e5m2, 14)}[fmt]
    v = np.moveaxis(np.asarray(x, np.float32).astype(ml_dtypes.bfloat16).astype(np.float64), axis, -1)
    blocks = v.reshape(v.shape[:-1] + (-1, 32))
    amax = np.abs(blocks).max(-1, keepdims=True)
    byte = np.maximum(np.where(amax > 0, np.frexp(amax)[1] - 1 + 127, 0) - down, 1)
    scale = np.exp2(byte - 127.0)
    codes = (blocks / scale).astype(np.float32).astype(dtype).astype(np.float64)
    return np.moveaxis((codes * scale).reshape(v.shape), -1, axis)


WIDE = False


def mx_kscale(k):
    if not WIDE:
        return np.ones(k)
    levels = np.array([10, -10, 5, -5, 0])
    a = np.random.permutation(np.resize(levels, k // 512 * 4)).reshape(k // 512, 4)
    idx = np.arange(k)
    return np.exp2(a[idx // 512, idx % 128 // 32])


BF16 = ml_dtypes.bfloat16


def bf(x):
    return np.asarray(x, np.float32).astype(BF16)


def f64(x):
    return np.asarray(x).astype(np.float64)


E2M1 = np.array([0.0, 0.5, 1.0, 1.5, 2.0, 3.0, 4.0, 6.0, -0.0, -0.5, -1.0, -1.5, -2.0, -3.0, -4.0, -6.0])


def pack_weight(w, fmt):
    k, n = w.shape
    w = f64(bf(w)).reshape(k // 32, 32, n)
    amax = np.abs(w).max(1)
    if fmt == "e4m3":
        byte = np.frexp(amax)[1] - 1 + 127 - 7
    else:
        mant, ex = np.frexp(amax / 6.0)
        byte = np.where(mant > 0.5, ex, ex - 1) + 127
    byte = np.clip(np.where(amax > 0, byte, 1), 1, 254)
    scaled = (w * np.exp2(127.0 - byte)[:, None, :]).reshape(k, n).astype(np.float32)
    by_word = np.ascontiguousarray(scaled.reshape(k // 512, 128, 4, n).transpose(0, 1, 3, 2))
    if fmt == "e4m3":
        words = by_word.astype(ml_dtypes.float8_e4m3fn).view(np.uint8)
    else:
        c = by_word.astype(ml_dtypes.float4_e2m1fn).view(np.uint8) & 0xF
        words = c[..., 0::2] | (c[..., 1::2] << 4)
    return np.ascontiguousarray(words), np.ascontiguousarray(byte.astype(np.uint8).reshape(k // 512, 16, n))


def unpack_weight(words, scales, fmt):
    g, p, n, _ = words.shape
    if fmt == "e4m3":
        vals = np.ascontiguousarray(words).view(ml_dtypes.float8_e4m3fn).astype(np.float64)
    else:
        nib = np.empty((g, p, n, 4), np.uint8)
        nib[..., 0::2] = words & 0xF
        nib[..., 1::2] = words >> 4
        vals = E2M1[nib]
    vals = vals * np.repeat(np.exp2(scales.astype(np.float64) - 127.0), 8, axis=1)[..., None]
    return vals.transpose(0, 1, 3, 2).reshape(g * 512, n)

def pack4(w):
    words, scales = pack_weight(w, "e2m1")
    return words.reshape(words.shape[0], 128, -1), scales


def unpack4(words, scales):
    return unpack_weight(words.reshape(words.shape[0], 128, -1, 2), scales, "e2m1")


B, D, E, H, W, SHIFT = 8, 1024, 512, 32, 32, 5
EPS = 1e-5


def erf(v):
    a = np.clip(v, -6.0, 6.0)
    a2 = 2.0 * a * a
    term = a.copy()
    tot = a.copy()
    for n in range(120):
        term = term * a2 / (2 * n + 3)
        tot = tot + term
    return 2.0 / np.sqrt(np.pi) * np.exp(-a * a) * tot


def gelu(v):
    return 0.5 * v * (1.0 + erf(v / np.sqrt(2.0)))


def conv1x1(x, w, b):
    n, c, hh, ww = x.shape
    y = w @ mxq(x.reshape(n, c, hh * ww), 1, "e4m3")
    return y.reshape(n, -1, hh, ww) + b[None, :, None, None]


def group_norm1(x, gamma, beta):
    m = x.mean(axis=(1, 2, 3), keepdims=True)
    v = x.var(axis=(1, 2, 3), keepdims=True)
    xh = (x - m) / np.sqrt(v + EPS)
    return xh * gamma[None, :, None, None] + beta[None, :, None, None]


def setup_inputs():
    s = mx_kscale(D)
    x = bf(np.random.standard_normal((B, D, H, W)) * s[None, :, None, None])
    w1 = np.random.standard_normal((E, D)) / np.sqrt(D) / s[None, :]
    w1_words, w1_scales = pack4(np.ascontiguousarray(w1.T))
    b1 = bf(np.random.standard_normal(E) * 0.3)
    g1 = bf(1.0 + 0.1 * np.random.standard_normal(E))
    be1 = bf(0.2 * np.random.standard_normal(E))
    return {"x": x,
            "w1_words": w1_words,
            "w1_scales": w1_scales,
            "b1": b1,
            "g1": g1,
            "be1": be1}


def reference(x, w1_words, w1_scales, b1, g1, be1):
    y = conv1x1(f64(x), unpack4(w1_words, w1_scales).T, f64(b1))
    return gelu(group_norm1(y, f64(g1), f64(be1)))

@@ -1,0 +1,244 @@
+from contextlib import ExitStack
+
+import concourse.mybir as mybir
+from concourse.masks import make_identity
+
+F32 = mybir.dt.float32
+BF16 = mybir.dt.bfloat16
+I32 = mybir.dt.int32
+U8 = mybir.dt.uint8
+U32 = mybir.dt.uint32
+FP8X4 = mybir.dt.float8_e4m3fn_x4
+FP4X4 = mybir.dt.float4_e2m1fn_x4
+ALU = mybir.AluOpType
+ACT = mybir.ActivationFunctionType
+
+P = 128
+PACK = 4
+SAMPLES = 8
+CHANNELS_IN = 1024
+CHANNELS_OUT = 512
+PIXELS = 1024
+EPS = 1e-5
+
+PASSES = CHANNELS_IN // (P * PACK)
+M_TILES = CHANNELS_OUT // P
+N_TILE = 512
+HALVES = PIXELS // N_TILE
+UNITS = M_TILES * HALVES
+
+VECTOR_COLUMNS = 384
+RUN = 4
+
+LOAD_LEAD = 5
+QUANTISE_LEAD = 3
+STATS_LEAD = 2
+COEFFICIENT_LEAD = 1
+
+FLOPS = 2 * SAMPLES * CHANNELS_OUT * CHANNELS_IN * PIXELS
+
+
+def tile_axialshift_pa_t_kernel(tc, x, w1_words, w1_scales, b1, g1, be1, out):
+    nc = tc.nc
+
+    x_chunks = x.rearrange("s (g p j) h w -> s g p j (h w)", g=PASSES, p=P, j=PACK)
+    out_tiles = out.rearrange("s (m p) h w -> s m p (h w)", p=P)
+
+    with ExitStack() as ctx:
+        consts = ctx.enter_context(tc.tile_pool(name="consts", bufs=1))
+        raw_pool = ctx.enter_context(tc.tile_pool(name="raw", bufs=6))
+        grouped_pool = ctx.enter_context(tc.tile_pool(name="grouped", bufs=3))
+        codes_pool = ctx.enter_context(tc.tile_pool(name="codes", bufs=4))
+        small_pool = ctx.enter_context(tc.tile_pool(name="small", bufs=4))
+        result_pool = ctx.enter_context(tc.tile_pool(name="result", bufs=6))
+        y_psum = ctx.enter_context(tc.psum_pool(name="y", bufs=7))
+        side_psum = ctx.enter_context(tc.psum_pool(name="side", bufs=1))
+
+        warm = consts.tile([P, 1], F32)
+        nc.vector.memset(warm[:], 0.0)
+        nc.scalar.activation(out=warm[:], in_=warm[:], func=ACT.Gelu)
+
+        w_words = consts.tile([P, PASSES, 2 * CHANNELS_OUT], U8, align_bytes=64)
+        w_scales = consts.tile([P, PASSES, CHANNELS_OUT], U8, align_bytes=64)
+        nc.vector.memset(w_scales[:].bitcast(I32), 0)
+
+        identity = consts.tile([P, P], BF16)
+        make_identity(nc, identity[:])
+        vector_rows = consts.tile([P, P], BF16)
+        nc.vector.memset(vector_rows[:], 0.0)
+
+        def load_constants():
+            for g in range(PASSES):
+                nc.sync.dma_start(out=w_words[:, g, :].bitcast(I32), in_=w1_words[g].bitcast(I32))
+            for quadrant in range(4):
+                nc.sync.dma_start(
+                    out=w_scales[32 * quadrant : 32 * quadrant + 4, :, :].bitcast(I32),
+                    in_=w1_scales[:, 4 * quadrant : 4 * quadrant + 4, :]
+                    .rearrange("g r n -> r g n")
+                    .bitcast(I32),
+                )
+            for i, vector in enumerate((b1, g1, be1)):
+                nc.sync.dma_start(
+                    out=vector_rows[M_TILES * i : M_TILES * (i + 1), :],
+                    in_=vector.rearrange("(m p) -> m p", p=P),
+                )
+
+        def spread_constants():
+            vector_columns = side_psum.tile([P, P], BF16, tag="side")
+            nc.tensor.transpose(vector_columns[:], vector_rows[:], identity[:])
+            nc.vector.tensor_copy(out=per_channel[:], in_=vector_columns[:, 0 : 3 * M_TILES])
+            nc.vector.tensor_copy(
+                out=bias_per_triple[:].rearrange("p (m r) -> p m r", m=M_TILES),
+                in_=bias.unsqueeze(2).to_broadcast([P, M_TILES, 2 * HALVES]),
+            )
+
+        per_channel = consts.tile([P, 3 * M_TILES], F32)
+        bias = per_channel[:, 0:M_TILES]
+        gamma = per_channel[:, M_TILES : 2 * M_TILES]
+        beta = per_channel[:, 2 * M_TILES : 3 * M_TILES]
+        bias_per_triple = consts.tile([P, 2 * UNITS], F32)
+
+        average = consts.tile([P, P], F32)
+        nc.vector.memset(average[:], 1.0 / P)
+        minus_half = consts.tile([P, 1], F32)
+        nc.vector.memset(minus_half[:], -0.5)
+
+        raw = {}
+        codes = {}
+        code_scales = {}
+        triples = {}
+        gains = {}
+        offsets = {}
+        results = {}
+
+        def exists(s):
+            return 0 <= s < SAMPLES
+
+        def load_sample(s):
+            if not exists(s):
+                return
+            for g in range(PASSES):
+                chunk = raw_pool.tile([P, PACK, PIXELS], BF16, tag="raw")
+                nc.sync.dma_start(out=chunk[:], in_=x_chunks[s, g])
+                raw[s, g] = chunk
+                if s == 0 and g == 0:
+                    load_constants()
+
+        def quantise_chunk(s, g):
+            if not exists(s):
+                return
+            if g == 0:
+                words = codes_pool.tile([P, PASSES, PIXELS], U32, tag="codes", align_bytes=64)
+                scale_bytes = codes_pool.tile([P, PASSES, PIXELS], U8, tag="scales", align_bytes=64)
+                codes[s] = words
+                code_scales[s] = scale_bytes
+            grouped = grouped_pool.tile([P, PIXELS, PACK], BF16, tag="grouped", align_bytes=64)
+            nc.vector.tensor_copy(
+                out=grouped[:, :VECTOR_COLUMNS, :].rearrange("p (c i) j -> p c j i", i=RUN),
+                in_=raw[s, g][:, :, :VECTOR_COLUMNS].rearrange("p j (c i) -> p c j i", i=RUN),
+            )
+            nc.scalar.copy(
+                out=grouped[:, VECTOR_COLUMNS:, :].rearrange("p (c i) j -> p c j i", i=RUN),
+                in_=raw[s, g][:, :, VECTOR_COLUMNS:].rearrange("p j (c i) -> p c j i", i=RUN),
+            )
+            nc.vector.quantize_mx(
+                out=codes[s][:, g, :].bitcast(FP8X4),
+                scales=code_scales[s][:, g, :],
+                in_=grouped[:].rearrange("p w j -> p (w j)"),
+            )
+
+        def multiply_unit(s, u):
+            m, half = divmod(u, HALVES)
+            pixels = slice(half * N_TILE, (half + 1) * N_TILE)
+            y = y_psum.tile([P, N_TILE], F32, tag="y")
+            for g in range(PASSES):
+                nc.tensor.matmul_mx(
+                    out=y[:],
+                    lhsT=w_words[:, g, 2 * P * m : 2 * P * (m + 1)].bitcast(FP4X4),
+                    lhsT_scale=w_scales[:, g, P * m : P * (m + 1)],
+                    rhs=codes[s][:, g, pixels].bitcast(FP8X4),
+                    rhs_scale=code_scales[s][:, g, pixels],
+                    start=(g == 0),
+                    stop=(g == PASSES - 1),
+                )
+            return y
+
+        def stats_unit(s, u):
+            if not exists(s):
+                return
+            if u == 0:
+                sample_triples = small_pool.tile([P, UNITS, 6], F32, tag="triples")
+                triples[s] = sample_triples
+            y = multiply_unit(s, u)
+            nc.vector.bn_stats(out=triples[s][:, u, :], in_=y[:])
+
+        def coefficients(s):
+            if not exists(s):
+                return
+            means = triples[s][:].rearrange("p u (e k) -> p (u e) k", k=3)[:, :, 1]
+            nc.vector.tensor_tensor(out=means, in0=means, in1=bias_per_triple[:], op=ALU.add)
+            moments = small_pool.tile([P, 2], F32, tag="moments")
+            nc.vector.bn_aggr(out=moments[:], in_=triples[s][:].rearrange("p u k -> p (u k)"))
+            nc.vector.scalar_tensor_tensor(
+                out=moments[:, 1:2],
+                in0=moments[:, 0:1],
+                scalar=moments[:, 0:1],
+                in1=moments[:, 1:2],
+                op0=ALU.mult,
+                op1=ALU.add,
+            )
+            sample_psum = side_psum.tile([P, 2], F32, tag="side")
+            nc.tensor.matmul(out=sample_psum[:], lhsT=average[:], rhs=moments[:], start=True, stop=True)
+            sample = small_pool.tile([P, 2], F32, tag="sample")
+            nc.vector.tensor_copy(out=sample[:], in_=sample_psum[:])
+            mean = sample[:, 0:1]
+            mean_of_squares = sample[:, 1:2]
+            work = small_pool.tile([P, 3 + M_TILES], F32, tag="work")
+            minus_variance = work[:, 0:1]
+            shifted_variance = work[:, 1:2]
+            inverse_deviation = work[:, 2:3]
+            centred_bias = work[:, 3 : 3 + M_TILES]
+            nc.gpsimd.tensor_scalar(
+                out=minus_variance, in0=mean, scalar1=mean, scalar2=mean_of_squares, op0=ALU.mult, op1=ALU.subtract
+            )
+            nc.gpsimd.tensor_scalar(
+                out=shifted_variance, in0=minus_variance, scalar1=-1.0, scalar2=EPS, op0=ALU.mult, op1=ALU.add
+            )
+            nc.gpsimd.tensor_tensor(out=inverse_deviation, in0=shifted_variance, in1=minus_half[:], op=ALU.pow)
+            gain = small_pool.tile([P, M_TILES], F32, tag="gain")
+            offset = small_pool.tile([P, M_TILES], F32, tag="offset")
+            nc.gpsimd.tensor_scalar(out=gain[:], in0=gamma, scalar1=inverse_deviation, scalar2=None, op0=ALU.mult)
+            nc.gpsimd.tensor_scalar(out=centred_bias, in0=bias, scalar1=mean, scalar2=None, op0=ALU.subtract)
+            nc.gpsimd.tensor_tensor(out=centred_bias, in0=centred_bias, in1=gain[:], op=ALU.mult)
+            nc.gpsimd.tensor_tensor(out=offset[:], in0=centred_bias, in1=beta, op=ALU.add)
+            gains[s] = gain
+            offsets[s] = offset
+
+        def output_unit(s, u):
+            if not exists(s):
+                return
+            m, half = divmod(u, HALVES)
+            if half == 0:
+                result = result_pool.tile([P, PIXELS], F32, tag="result")
+                results[s, m] = result
+            y = multiply_unit(s, u)
+            nc.scalar.activation(
+                out=results[s, m][:, half * N_TILE : (half + 1) * N_TILE],
+                in_=y[:],
+                func=ACT.Gelu,
+                bias=offsets[s][:, m : m + 1],
+                scale=gains[s][:, m : m + 1],
+            )
+            if half == HALVES - 1:
+                nc.sync.dma_start(out=out_tiles[s, m], in_=results[s, m][:])
+
+        for t in range(-LOAD_LEAD, SAMPLES):
+            load_sample(t + LOAD_LEAD)
+            if t == -LOAD_LEAD:
+                spread_constants()
+            coefficients(t + COEFFICIENT_LEAD)
+            for u in range(UNITS):
+                if u % (UNITS // PASSES) == 0:
+                    quantise_chunk(t + QUANTISE_LEAD, u // (UNITS // PASSES))
+                stats_unit(t + STATS_LEAD, u)
+                output_unit(t, u)

@@ -27,7 +27,7 @@ N_TILE = 512
 HALVES = PIXELS // N_TILE
 UNITS = M_TILES * HALVES
 
-VECTOR_COLUMNS = 384
+VECTOR_COLUMNS = 320
 RUN = 4
 
 LOAD_LEAD = 5

@@ -27,13 +27,12 @@ N_TILE = 512
 HALVES = PIXELS // N_TILE
 UNITS = M_TILES * HALVES
 
-VECTOR_COLUMNS = 320
+VECTOR_COLUMNS = 256
+GPSIMD_COLUMNS = 192
+SCALAR_END = PIXELS - GPSIMD_COLUMNS
 RUN = 4
 
-LOAD_LEAD = 5
-QUANTISE_LEAD = 3
-STATS_LEAD = 2
-COEFFICIENT_LEAD = 1
+GELU_LAG = 1
 
 FLOPS = 2 * SAMPLES * CHANNELS_OUT * CHANNELS_IN * PIXELS
 
@@ -46,11 +45,11 @@ def tile_axialshift_pa_t_kernel(tc, x, w1_words, w1_scales, b1, g1, be1, out):
 
     with ExitStack() as ctx:
         consts = ctx.enter_context(tc.tile_pool(name="consts", bufs=1))
-        raw_pool = ctx.enter_context(tc.tile_pool(name="raw", bufs=6))
-        grouped_pool = ctx.enter_context(tc.tile_pool(name="grouped", bufs=3))
-        codes_pool = ctx.enter_context(tc.tile_pool(name="codes", bufs=4))
-        small_pool = ctx.enter_context(tc.tile_pool(name="small", bufs=4))
-        result_pool = ctx.enter_context(tc.tile_pool(name="result", bufs=6))
+        raw_pool = ctx.enter_context(tc.tile_pool(name="raw", bufs=8))
+        grouped_pool = ctx.enter_context(tc.tile_pool(name="grouped", bufs=4))
+        codes_pool = ctx.enter_context(tc.tile_pool(name="codes", bufs=8))
+        small_pool = ctx.enter_context(tc.tile_pool(name="small", bufs=8))
+        result_pool = ctx.enter_context(tc.tile_pool(name="result", bufs=8))
         y_psum = ctx.enter_context(tc.psum_pool(name="y", bufs=7))
         side_psum = ctx.enter_context(tc.psum_pool(name="side", bufs=1))
 
@@ -138,8 +137,16 @@ def tile_axialshift_pa_t_kernel(tc, x, w1_words, w1_scales, b1, g1, be1, out):
                 in_=raw[s, g][:, :, :VECTOR_COLUMNS].rearrange("p j (c i) -> p c j i", i=RUN),
             )
             nc.scalar.copy(
-                out=grouped[:, VECTOR_COLUMNS:, :].rearrange("p (c i) j -> p c j i", i=RUN),
-                in_=raw[s, g][:, :, VECTOR_COLUMNS:].rearrange("p j (c i) -> p c j i", i=RUN),
+                out=grouped[:, VECTOR_COLUMNS:SCALAR_END, :].rearrange("p (c i) j -> p c j i", i=RUN),
+                in_=raw[s, g][:, :, VECTOR_COLUMNS:SCALAR_END].rearrange("p j (c i) -> p c j i", i=RUN),
+            )
+            nc.gpsimd.tensor_scalar(
+                out=grouped[:, SCALAR_END:, :].rearrange("p (c i) j -> p c j i", i=RUN),
+                in0=raw[s, g][:, :, SCALAR_END:].rearrange("p j (c i) -> p c j i", i=RUN),
+                scalar1=1.0,
+                scalar2=0.0,
+                op0=ALU.mult,
+                op1=ALU.add,
             )
             nc.vector.quantize_mx(
                 out=codes[s][:, g, :].bitcast(FP8X4),
@@ -232,13 +239,14 @@ def tile_axialshift_pa_t_kernel(tc, x, w1_words, w1_scales, b1, g1, be1, out):
             if half == HALVES - 1:
                 nc.sync.dma_start(out=out_tiles[s, m], in_=results[s, m][:])
 
-        for t in range(-LOAD_LEAD, SAMPLES):
-            load_sample(t + LOAD_LEAD)
-            if t == -LOAD_LEAD:
+        for t in range(SAMPLES + GELU_LAG):
+            load_sample(t)
+            if t == 0:
                 spread_constants()
-            coefficients(t + COEFFICIENT_LEAD)
+            for g in range(PASSES):
+                quantise_chunk(t, g)
             for u in range(UNITS):
-                if u % (UNITS // PASSES) == 0:
-                    quantise_chunk(t + QUANTISE_LEAD, u // (UNITS // PASSES))
-                stats_unit(t + STATS_LEAD, u)
-                output_unit(t, u)
+                stats_unit(t, u)
+            coefficients(t)
+            for u in range(UNITS):
+                output_unit(t - GELU_LAG, u)

@@ -26,15 +26,29 @@ M_TILES = CHANNELS_OUT // P
 N_TILE = 512
 HALVES = PIXELS // N_TILE
 UNITS = M_TILES * HALVES
-
-VECTOR_COLUMNS = 256
-GPSIMD_COLUMNS = 192
-SCALAR_END = PIXELS - GPSIMD_COLUMNS
+BANKS = 8
 RUN = 4
 
-GELU_LAG = 1
+
+FIRST_ORDER = (1, 2, 3, 0)
+
+LOADS_AHEAD = 4
+RAW_BUFS = 2 * LOADS_AHEAD
+
+FIRST_PLAN = {
+    (0, 0): [("V", 256), ("S", 256)], (1, 0): [("V", 256), ("S", 256)],
+    (0, 1): [("V", 256), ("S", 256)], (1, 1): [("V", 256), ("S", 256)],
+}
+PLAN = {
+    (0, 0): [("V", 192), ("S", 320)], (1, 0): [("V", 192), ("S", 320)],
+    (0, 1): [("G", 416), ("S", 96)], (1, 1): [("G", 416), ("S", 96)],
+}
 
 FLOPS = 2 * SAMPLES * CHANNELS_OUT * CHANNELS_IN * PIXELS
+
+
+def plan_of(s):
+    return FIRST_PLAN if s == 0 else PLAN
 
 
 def tile_axialshift_pa_t_kernel(tc, x, w1_words, w1_scales, b1, g1, be1, out):
@@ -45,13 +59,17 @@ def tile_axialshift_pa_t_kernel(tc, x, w1_words, w1_scales, b1, g1, be1, out):
 
     with ExitStack() as ctx:
         consts = ctx.enter_context(tc.tile_pool(name="consts", bufs=1))
-        raw_pool = ctx.enter_context(tc.tile_pool(name="raw", bufs=8))
-        grouped_pool = ctx.enter_context(tc.tile_pool(name="grouped", bufs=4))
-        codes_pool = ctx.enter_context(tc.tile_pool(name="codes", bufs=8))
-        small_pool = ctx.enter_context(tc.tile_pool(name="small", bufs=8))
+        raw_pool = ctx.enter_context(tc.tile_pool(name="raw", bufs=RAW_BUFS))
+        stage_pool = ctx.enter_context(tc.tile_pool(name="stage", bufs=1))
+        codes_pool = ctx.enter_context(tc.tile_pool(name="codes", bufs=3))
+        small_pool = ctx.enter_context(tc.tile_pool(name="small", bufs=3))
         result_pool = ctx.enter_context(tc.tile_pool(name="result", bufs=8))
-        y_psum = ctx.enter_context(tc.psum_pool(name="y", bufs=7))
-        side_psum = ctx.enter_context(tc.psum_pool(name="side", bufs=1))
+        psum = ctx.enter_context(tc.psum_pool(name="psum", bufs=1))
+        ctx.enter_context(tc.manual_schedule())
+
+        def bank_tile(b, shape, dtype):
+            bank = psum.tile(shape, dtype, tag="bank%d" % b, name="bank%d" % b)
+            return bank
 
         warm = consts.tile([P, 1], F32)
         nc.vector.memset(warm[:], 0.0)
@@ -60,15 +78,26 @@ def tile_axialshift_pa_t_kernel(tc, x, w1_words, w1_scales, b1, g1, be1, out):
         w_words = consts.tile([P, PASSES, 2 * CHANNELS_OUT], U8, align_bytes=64)
         w_scales = consts.tile([P, PASSES, CHANNELS_OUT], U8, align_bytes=64)
         nc.vector.memset(w_scales[:].bitcast(I32), 0)
-
         identity = consts.tile([P, P], BF16)
         make_identity(nc, identity[:])
         vector_rows = consts.tile([P, P], BF16)
         nc.vector.memset(vector_rows[:], 0.0)
+        average = consts.tile([P, P], F32)
+        nc.vector.memset(average[:], 1.0 / P)
+        minus_half = consts.tile([P, 1], F32)
+        nc.vector.memset(minus_half[:], -0.5)
+        per_channel = consts.tile([P, 3 * M_TILES], F32)
+        bias = per_channel[:, 0:M_TILES]
+        gamma = per_channel[:, M_TILES : 2 * M_TILES]
+        bias_per_triple = consts.tile([P, 2 * UNITS], F32)
+        factors = consts.tile([P, 2 * M_TILES], F32)
+        addends = consts.tile([P, 2 * M_TILES], F32)
+        nc.vector.memset(addends[:], 0.0)
 
         def load_constants():
-            for g in range(PASSES):
-                nc.sync.dma_start(out=w_words[:, g, :].bitcast(I32), in_=w1_words[g].bitcast(I32))
+            nc.sync.dma_start(
+                out=w_words[:].bitcast(I32), in_=w1_words.rearrange("g p n -> p g n").bitcast(I32)
+            )
             for quadrant in range(4):
                 nc.sync.dma_start(
                     out=w_scales[32 * quadrant : 32 * quadrant + 4, :, :].bitcast(I32),
@@ -76,6 +105,8 @@ def tile_axialshift_pa_t_kernel(tc, x, w1_words, w1_scales, b1, g1, be1, out):
                     .rearrange("g r n -> r g n")
                     .bitcast(I32),
                 )
+
+        def load_vectors():
             for i, vector in enumerate((b1, g1, be1)):
                 nc.sync.dma_start(
                     out=vector_rows[M_TILES * i : M_TILES * (i + 1), :],
@@ -83,81 +114,137 @@ def tile_axialshift_pa_t_kernel(tc, x, w1_words, w1_scales, b1, g1, be1, out):
                 )
 
         def spread_constants():
-            vector_columns = side_psum.tile([P, P], BF16, tag="side")
+            vector_columns = bank_tile(M_TILES + 1, [P, P], BF16)
             nc.tensor.transpose(vector_columns[:], vector_rows[:], identity[:])
             nc.vector.tensor_copy(out=per_channel[:], in_=vector_columns[:, 0 : 3 * M_TILES])
             nc.vector.tensor_copy(
                 out=bias_per_triple[:].rearrange("p (m r) -> p m r", m=M_TILES),
                 in_=bias.unsqueeze(2).to_broadcast([P, M_TILES, 2 * HALVES]),
             )
-
-        per_channel = consts.tile([P, 3 * M_TILES], F32)
-        bias = per_channel[:, 0:M_TILES]
-        gamma = per_channel[:, M_TILES : 2 * M_TILES]
-        beta = per_channel[:, 2 * M_TILES : 3 * M_TILES]
-        bias_per_triple = consts.tile([P, 2 * UNITS], F32)
-
-        average = consts.tile([P, P], F32)
-        nc.vector.memset(average[:], 1.0 / P)
-        minus_half = consts.tile([P, 1], F32)
-        nc.vector.memset(minus_half[:], -0.5)
+            nc.vector.tensor_copy(out=factors[:, 0:M_TILES], in_=gamma)
+            nc.vector.tensor_copy(out=addends[:, M_TILES:], in_=per_channel[:, 2 * M_TILES : 3 * M_TILES])
 
         raw = {}
+        staged = {}
         codes = {}
         code_scales = {}
         triples = {}
-        gains = {}
-        offsets = {}
+        coefficients = {}
         results = {}
+        bank_of = {}
+        y_tiles = {}
 
         def exists(s):
             return 0 <= s < SAMPLES
 
-        def load_sample(s):
+        def load_sample(s, split):
             if not exists(s):
                 return
             for g in range(PASSES):
                 chunk = raw_pool.tile([P, PACK, PIXELS], BF16, tag="raw")
-                nc.sync.dma_start(out=chunk[:], in_=x_chunks[s, g])
                 raw[s, g] = chunk
-                if s == 0 and g == 0:
-                    load_constants()
+            if split:
+                for half in range(HALVES):
+                    for g in range(PASSES):
+                        cols = slice(half * N_TILE, (half + 1) * N_TILE)
+                        nc.sync.dma_start(out=raw[s, g][:, :, cols], in_=x_chunks[s, g][:, :, cols])
+                    if half == 0:
+                        load_constants()
+            else:
+                for g in range(PASSES):
+                    nc.sync.dma_start(out=raw[s, g][:], in_=x_chunks[s, g])
 
-        def quantise_chunk(s, g):
+        def stage_of(s, g, half):
+            if (s, g, half) not in staged:
+                if half == 0:
+                    stage = stage_pool.tile([P, N_TILE, PACK], BF16, tag="first", bufs=3 * PASSES, align_bytes=64)
+                else:
+                    stage = stage_pool.tile(
+                        [P, N_TILE, PACK], BF16, tag="second%d" % g, bufs=1, align_bytes=64, name="second%d" % g
+                    )
+                staged[s, g, half] = stage
+            return staged[s, g, half]
+
+        def parts_of(s, g, half, engine):
+            first = 0
+            found = []
+            for who, width in plan_of(s)[g, half]:
+                if who == engine:
+                    found.append((first, width))
+                first += width
+            return found
+
+        def regroup_part(s, g, half, engine):
+            for first, width in parts_of(s, g, half, engine):
+                target = stage_of(s, g, half)[:, first : first + width, :]
+                source = raw[s, g][:, :, half * N_TILE + first : half * N_TILE + first + width]
+                if engine == "V":
+                    nc.vector.tensor_copy(
+                        out=target.rearrange("p (c i) j -> p c j i", i=RUN),
+                        in_=source.rearrange("p j (c i) -> p c j i", i=RUN),
+                    )
+                elif engine == "S":
+                    nc.scalar.copy(
+                        out=target.rearrange("p (c i) j -> p c j i", i=RUN),
+                        in_=source.rearrange("p j (c i) -> p c j i", i=RUN),
+                    )
+                else:
+                    nc.gpsimd.tensor_scalar(
+                        out=target,
+                        in0=source.rearrange("p j w -> p w j"),
+                        scalar1=1.0,
+                        scalar2=0.0,
+                        op0=ALU.mult,
+                        op1=ALU.add,
+                    )
+
+        def regroup(s, engine):
             if not exists(s):
                 return
-            if g == 0:
+            for half in range(HALVES):
+                for g in range(PASSES):
+                    regroup_part(s, g, half, engine)
+
+        turned = {}
+
+        def turn(s, g, half, b):
+            for first, width in parts_of(s, g, half, "T"):
+                bank = bank_tile(b, [P, width * PACK], BF16)
+                for c in range(0, width, N_TILE // PACK):
+                    cols = slice(half * N_TILE + first + c, half * N_TILE + first + c + N_TILE // PACK)
+                    nc.tensor.matmul(
+                        out=bank[:, c * PACK : c * PACK + N_TILE],
+                        lhsT=identity[:],
+                        rhs=raw[s, g][:, :, cols].rearrange("p j w -> p w j"),
+                        start=True,
+                        stop=True,
+                    )
+                turned[s, g, half] = bank
+
+        def fetch(s, g, half):
+            for first, width in parts_of(s, g, half, "T"):
+                nc.scalar.copy(
+                    out=stage_of(s, g, half)[:, first : first + width, :].rearrange("p w j -> p (w j)"),
+                    in_=turned[s, g, half][:],
+                )
+
+        def quantise_block(s, g, half):
+            if s not in codes:
                 words = codes_pool.tile([P, PASSES, PIXELS], U32, tag="codes", align_bytes=64)
                 scale_bytes = codes_pool.tile([P, PASSES, PIXELS], U8, tag="scales", align_bytes=64)
                 codes[s] = words
                 code_scales[s] = scale_bytes
-            grouped = grouped_pool.tile([P, PIXELS, PACK], BF16, tag="grouped", align_bytes=64)
-            nc.vector.tensor_copy(
-                out=grouped[:, :VECTOR_COLUMNS, :].rearrange("p (c i) j -> p c j i", i=RUN),
-                in_=raw[s, g][:, :, :VECTOR_COLUMNS].rearrange("p j (c i) -> p c j i", i=RUN),
-            )
-            nc.scalar.copy(
-                out=grouped[:, VECTOR_COLUMNS:SCALAR_END, :].rearrange("p (c i) j -> p c j i", i=RUN),
-                in_=raw[s, g][:, :, VECTOR_COLUMNS:SCALAR_END].rearrange("p j (c i) -> p c j i", i=RUN),
-            )
-            nc.gpsimd.tensor_scalar(
-                out=grouped[:, SCALAR_END:, :].rearrange("p (c i) j -> p c j i", i=RUN),
-                in0=raw[s, g][:, :, SCALAR_END:].rearrange("p j (c i) -> p c j i", i=RUN),
-                scalar1=1.0,
-                scalar2=0.0,
-                op0=ALU.mult,
-                op1=ALU.add,
-            )
+            pixels = slice(half * N_TILE, (half + 1) * N_TILE)
             nc.vector.quantize_mx(
-                out=codes[s][:, g, :].bitcast(FP8X4),
-                scales=code_scales[s][:, g, :],
-                in_=grouped[:].rearrange("p w j -> p (w j)"),
+                out=codes[s][:, g, pixels].bitcast(FP8X4),
+                scales=code_scales[s][:, g, pixels],
+                in_=staged[s, g, half][:].rearrange("p w j -> p (w j)"),
             )
 
-        def multiply_unit(s, u):
-            m, half = divmod(u, HALVES)
+        def multiply(s, unit, b):
+            m, half = unit
             pixels = slice(half * N_TILE, (half + 1) * N_TILE)
-            y = y_psum.tile([P, N_TILE], F32, tag="y")
+            y = bank_tile(b, [P, N_TILE], F32)
             for g in range(PASSES):
                 nc.tensor.matmul_mx(
                     out=y[:],
@@ -168,85 +255,140 @@ def tile_axialshift_pa_t_kernel(tc, x, w1_words, w1_scales, b1, g1, be1, out):
                     start=(g == 0),
                     stop=(g == PASSES - 1),
                 )
-            return y
+            y_tiles[s, unit] = y
+            bank_of[s, unit] = b
 
-        def stats_unit(s, u):
-            if not exists(s):
-                return
-            if u == 0:
+        def statistics(s, unit):
+            if s not in triples:
                 sample_triples = small_pool.tile([P, UNITS, 6], F32, tag="triples")
                 triples[s] = sample_triples
-            y = multiply_unit(s, u)
-            nc.vector.bn_stats(out=triples[s][:, u, :], in_=y[:])
+            m, half = unit
+            nc.vector.bn_stats(out=triples[s][:, HALVES * m + half, :], in_=y_tiles[s, unit][:])
 
-        def coefficients(s):
-            if not exists(s):
-                return
+        def gelu(s, unit):
+            m, half = unit
+            if (s, m) not in results:
+                result = result_pool.tile([P, PIXELS], F32, tag="result")
+                results[s, m] = [result, 0]
+            nc.scalar.activation(
+                out=results[s, m][0][:, half * N_TILE : (half + 1) * N_TILE],
+                in_=y_tiles[s, unit][:],
+                func=ACT.Gelu,
+                bias=coefficients[s][:, M_TILES + m : M_TILES + m + 1],
+                scale=coefficients[s][:, m : m + 1],
+            )
+            results[s, m][1] += 1
+            if results[s, m][1] == HALVES:
+                nc.sync.dma_start(out=out_tiles[s, m], in_=results[s, m][0][:])
+
+        def chain(s, fillers):
+            def fill(n):
+                for i in range(n):
+                    if fillers:
+                        fillers.pop(0)()
+
             means = triples[s][:].rearrange("p u (e k) -> p (u e) k", k=3)[:, :, 1]
             nc.vector.tensor_tensor(out=means, in0=means, in1=bias_per_triple[:], op=ALU.add)
+            fill(1)
             moments = small_pool.tile([P, 2], F32, tag="moments")
             nc.vector.bn_aggr(out=moments[:], in_=triples[s][:].rearrange("p u k -> p (u k)"))
-            nc.vector.scalar_tensor_tensor(
-                out=moments[:, 1:2],
-                in0=moments[:, 0:1],
-                scalar=moments[:, 0:1],
-                in1=moments[:, 1:2],
-                op0=ALU.mult,
-                op1=ALU.add,
+            fill(1)
+            nc.vector.tensor_scalar(
+                out=moments[:, 1:2], in0=moments[:, 0:1], scalar1=moments[:, 0:1], scalar2=moments[:, 1:2],
+                op0=ALU.mult, op1=ALU.add,
             )
-            sample_psum = side_psum.tile([P, 2], F32, tag="side")
-            nc.tensor.matmul(out=sample_psum[:], lhsT=average[:], rhs=moments[:], start=True, stop=True)
-            sample = small_pool.tile([P, 2], F32, tag="sample")
-            nc.vector.tensor_copy(out=sample[:], in_=sample_psum[:])
+            sample = bank_tile(M_TILES, [P, 2], F32)
+            nc.tensor.matmul(out=sample[:], lhsT=average[:], rhs=moments[:], start=True, stop=True)
+            fill(1)
             mean = sample[:, 0:1]
             mean_of_squares = sample[:, 1:2]
-            work = small_pool.tile([P, 3 + M_TILES], F32, tag="work")
-            minus_variance = work[:, 0:1]
-            shifted_variance = work[:, 1:2]
-            inverse_deviation = work[:, 2:3]
-            centred_bias = work[:, 3 : 3 + M_TILES]
-            nc.gpsimd.tensor_scalar(
-                out=minus_variance, in0=mean, scalar1=mean, scalar2=mean_of_squares, op0=ALU.mult, op1=ALU.subtract
+            work = small_pool.tile([P, 3], F32, tag="work")
+            nc.vector.tensor_scalar(
+                out=work[:, 0:1], in0=mean, scalar1=mean, scalar2=mean_of_squares, op0=ALU.mult, op1=ALU.subtract
+            )
+            nc.vector.scalar_tensor_tensor(
+                out=factors[:, M_TILES:], in0=bias, scalar=mean, in1=gamma, op0=ALU.subtract, op1=ALU.mult
             )
             nc.gpsimd.tensor_scalar(
-                out=shifted_variance, in0=minus_variance, scalar1=-1.0, scalar2=EPS, op0=ALU.mult, op1=ALU.add
+                out=work[:, 1:2], in0=work[:, 0:1], scalar1=-1.0, scalar2=EPS, op0=ALU.mult, op1=ALU.add
             )
-            nc.gpsimd.tensor_tensor(out=inverse_deviation, in0=shifted_variance, in1=minus_half[:], op=ALU.pow)
-            gain = small_pool.tile([P, M_TILES], F32, tag="gain")
-            offset = small_pool.tile([P, M_TILES], F32, tag="offset")
-            nc.gpsimd.tensor_scalar(out=gain[:], in0=gamma, scalar1=inverse_deviation, scalar2=None, op0=ALU.mult)
-            nc.gpsimd.tensor_scalar(out=centred_bias, in0=bias, scalar1=mean, scalar2=None, op0=ALU.subtract)
-            nc.gpsimd.tensor_tensor(out=centred_bias, in0=centred_bias, in1=gain[:], op=ALU.mult)
-            nc.gpsimd.tensor_tensor(out=offset[:], in0=centred_bias, in1=beta, op=ALU.add)
-            gains[s] = gain
-            offsets[s] = offset
-
-        def output_unit(s, u):
-            if not exists(s):
-                return
-            m, half = divmod(u, HALVES)
-            if half == 0:
-                result = result_pool.tile([P, PIXELS], F32, tag="result")
-                results[s, m] = result
-            y = multiply_unit(s, u)
-            nc.scalar.activation(
-                out=results[s, m][:, half * N_TILE : (half + 1) * N_TILE],
-                in_=y[:],
-                func=ACT.Gelu,
-                bias=offsets[s][:, m : m + 1],
-                scale=gains[s][:, m : m + 1],
+            nc.gpsimd.tensor_tensor(out=work[:, 2:3], in0=work[:, 1:2], in1=minus_half[:], op=ALU.pow)
+            fill(1)
+            pair = small_pool.tile([P, 2 * M_TILES], F32, tag="pair")
+            nc.vector.scalar_tensor_tensor(
+                out=pair[:], in0=factors[:], scalar=work[:, 2:3], in1=addends[:], op0=ALU.mult, op1=ALU.add
             )
-            if half == HALVES - 1:
-                nc.sync.dma_start(out=out_tiles[s, m], in_=results[s, m][:])
+            coefficients[s] = pair
+            fill(len(fillers))
 
-        for t in range(SAMPLES + GELU_LAG):
-            load_sample(t)
-            if t == 0:
-                spread_constants()
+        def quantiser(s, g, half):
+            return lambda: quantise_block(s, g, half)
+
+        def regrouper(s, g, half):
+            return lambda: regroup_part(s, g, half, "V")
+
+        def vector_work(k):
+            calls = []
+            if exists(k + 1):
+                calls += [regrouper(k + 1, g, 0) for g in range(PASSES)]
+                calls += [quantiser(k + 1, g, 0) for g in range(PASSES)]
+            return calls
+
+        load_sample(0, split=True)
+        load_sample(1, split=False)
+        load_vectors()
+        for s in range(2, LOADS_AHEAD):
+            load_sample(s, split=False)
+        for half in range(HALVES):
             for g in range(PASSES):
-                quantise_chunk(t, g)
-            for u in range(UNITS):
-                stats_unit(t, u)
-            coefficients(t)
-            for u in range(UNITS):
-                output_unit(t - GELU_LAG, u)
+                regroup_part(0, g, half, "V")
+                regroup_part(0, g, half, "S")
+            if half == 0:
+                for g in range(PASSES):
+                    quantise_block(0, g, half)
+                for m in FIRST_ORDER:
+                    multiply(0, (m, 0), M_TILES + m)
+        for g in range(PASSES):
+            regroup_part(1, g, 0, "S")
+
+        for k in range(SAMPLES + 1):
+            load_sample(k + LOADS_AHEAD, split=False)
+            if exists(k):
+                for g in reversed(range(PASSES)):
+                    quantise_block(k, g, 1)
+            regroup(k + 1, "G")
+            if k == SAMPLES:
+                for m in range(M_TILES):
+                    multiply(k - 1, (m, 0), M_TILES + m)
+                for m in range(M_TILES):
+                    gelu(k - 1, (m, 1))
+                    gelu(k - 1, (m, 0))
+                break
+            for m in range(M_TILES):
+                if exists(k - 1):
+                    gelu(k - 1, (m, 1))
+                if exists(k):
+                    multiply(k, (m, 1), m)
+            if exists(k):
+                for m in FIRST_ORDER:
+                    statistics(k, (m, 0))
+                for m in range(M_TILES):
+                    statistics(k, (m, 1))
+            if exists(k + 1):
+                for g in range(PASSES):
+                    regroup_part(k + 1, g, 1, "S")
+            if exists(k + 2):
+                regroup_part(k + 2, 0, 0, "S")
+            for m in range(M_TILES):
+                if exists(k - 1):
+                    multiply(k - 1, (m, 0), M_TILES + m)
+                    gelu(k - 1, (m, 0))
+            if exists(k + 2):
+                regroup_part(k + 2, 1, 0, "S")
+            if k == 0:
+                spread_constants()
+            if exists(k):
+                chain(k, vector_work(k))
+            if exists(k + 1):
+                for m in FIRST_ORDER:
+                    multiply(k + 1, (m, 0), M_TILES + m)

@@ -184,10 +184,7 @@ def tile_axialshift_pa_t_kernel(tc, x, w1_words, w1_scales, b1, g1, be1, out):
                         in_=source.rearrange("p j (c i) -> p c j i", i=RUN),
                     )
                 elif engine == "S":
-                    nc.scalar.copy(
-                        out=target.rearrange("p (c i) j -> p c j i", i=RUN),
-                        in_=source.rearrange("p j (c i) -> p c j i", i=RUN),
-                    )
+                    nc.scalar.copy(out=target, in_=source.rearrange("p j w -> p w j"))
                 else:
                     nc.gpsimd.tensor_scalar(
                         out=target,

@@ -41,7 +41,7 @@ FIRST_PLAN = {
 }
 PLAN = {
     (0, 0): [("V", 192), ("S", 320)], (1, 0): [("V", 192), ("S", 320)],
-    (0, 1): [("G", 416), ("S", 96)], (1, 1): [("G", 416), ("S", 96)],
+    (0, 1): [("G", 320), ("S", 192)], (1, 1): [("G", 320), ("S", 192)],
 }
 
 FLOPS = 2 * SAMPLES * CHANNELS_OUT * CHANNELS_IN * PIXELS

@@ -40,8 +40,8 @@ FIRST_PLAN = {
     (0, 1): [("V", 256), ("S", 256)], (1, 1): [("V", 256), ("S", 256)],
 }
 PLAN = {
-    (0, 0): [("V", 192), ("S", 320)], (1, 0): [("V", 192), ("S", 320)],
-    (0, 1): [("G", 320), ("S", 192)], (1, 1): [("G", 320), ("S", 192)],
+    (0, 0): [("V", 96), ("S", 416)], (1, 0): [("V", 96), ("S", 416)],
+    (0, 1): [("G", 416), ("S", 96)], (1, 1): [("G", 416), ("S", 96)],
 }
 
 FLOPS = 2 * SAMPLES * CHANNELS_OUT * CHANNELS_IN * PIXELS

@@ -40,7 +40,7 @@ FIRST_PLAN = {
     (0, 1): [("V", 256), ("S", 256)], (1, 1): [("V", 256), ("S", 256)],
 }
 PLAN = {
-    (0, 0): [("V", 96), ("S", 416)], (1, 0): [("V", 96), ("S", 416)],
+    (0, 0): [("S", 512)], (1, 0): [("V", 192), ("S", 320)],
     (0, 1): [("G", 416), ("S", 96)], (1, 1): [("G", 416), ("S", 96)],
 }
 
@@ -84,12 +84,19 @@ def tile_axialshift_pa_t_kernel(tc, x, w1_words, w1_scales, b1, g1, be1, out):
         nc.vector.memset(vector_rows[:], 0.0)
         average = consts.tile([P, P], F32)
         nc.vector.memset(average[:], 1.0 / P)
+        minus_average = consts.tile([P, P], F32)
+        nc.vector.memset(minus_average[:], -1.0 / P)
         minus_half = consts.tile([P, 1], F32)
         nc.vector.memset(minus_half[:], -0.5)
         per_channel = consts.tile([P, 3 * M_TILES], F32)
         bias = per_channel[:, 0:M_TILES]
         gamma = per_channel[:, M_TILES : 2 * M_TILES]
-        bias_per_triple = consts.tile([P, 2 * UNITS], F32)
+        shift_per_triple = consts.tile([P, 2 * UNITS, 2], F32)
+        nc.vector.memset(shift_per_triple[:], 0.0)
+        nc.vector.tensor_scalar(
+            out=shift_per_triple[:, :, 1], in0=shift_per_triple[:, :, 1], scalar1=EPS * N_TILE / 2, scalar2=None,
+            op0=ALU.add,
+        )
         factors = consts.tile([P, 2 * M_TILES], F32)
         addends = consts.tile([P, 2 * M_TILES], F32)
         nc.vector.memset(addends[:], 0.0)
@@ -118,7 +125,7 @@ def tile_axialshift_pa_t_kernel(tc, x, w1_words, w1_scales, b1, g1, be1, out):
             nc.tensor.transpose(vector_columns[:], vector_rows[:], identity[:])
             nc.vector.tensor_copy(out=per_channel[:], in_=vector_columns[:, 0 : 3 * M_TILES])
             nc.vector.tensor_copy(
-                out=bias_per_triple[:].rearrange("p (m r) -> p m r", m=M_TILES),
+                out=shift_per_triple[:, :, 0].rearrange("p (m r) -> p m r", m=M_TILES),
                 in_=bias.unsqueeze(2).to_broadcast([P, M_TILES, 2 * HALVES]),
             )
             nc.vector.tensor_copy(out=factors[:, 0:M_TILES], in_=gamma)
@@ -154,16 +161,14 @@ def tile_axialshift_pa_t_kernel(tc, x, w1_words, w1_scales, b1, g1, be1, out):
                 for g in range(PASSES):
                     nc.sync.dma_start(out=raw[s, g][:], in_=x_chunks[s, g])
 
-        def stage_of(s, g, half):
-            if (s, g, half) not in staged:
+        def stage_of(s, half):
+            if (s, half) not in staged:
                 if half == 0:
-                    stage = stage_pool.tile([P, N_TILE, PACK], BF16, tag="first", bufs=3 * PASSES, align_bytes=64)
+                    stage = stage_pool.tile([P, PASSES, N_TILE, PACK], BF16, tag="first", bufs=3, align_bytes=64)
                 else:
-                    stage = stage_pool.tile(
-                        [P, N_TILE, PACK], BF16, tag="second%d" % g, bufs=1, align_bytes=64, name="second%d" % g
-                    )
-                staged[s, g, half] = stage
-            return staged[s, g, half]
+                    stage = stage_pool.tile([P, PASSES, N_TILE, PACK], BF16, tag="second", bufs=1, align_bytes=64)
+                staged[s, half] = stage
+            return staged[s, half]
 
         def parts_of(s, g, half, engine):
             first = 0
@@ -176,7 +181,7 @@ def tile_axialshift_pa_t_kernel(tc, x, w1_words, w1_scales, b1, g1, be1, out):
 
         def regroup_part(s, g, half, engine):
             for first, width in parts_of(s, g, half, engine):
-                target = stage_of(s, g, half)[:, first : first + width, :]
+                target = stage_of(s, half)[:, g, first : first + width, :]
                 source = raw[s, g][:, :, half * N_TILE + first : half * N_TILE + first + width]
                 if engine == "V":
                     nc.vector.tensor_copy(
@@ -225,30 +230,28 @@ def tile_axialshift_pa_t_kernel(tc, x, w1_words, w1_scales, b1, g1, be1, out):
                     in_=turned[s, g, half][:],
                 )
 
-        def quantise_block(s, g, half):
+        def quantise_half(s, half):
             if s not in codes:
-                words = codes_pool.tile([P, PASSES, PIXELS], U32, tag="codes", align_bytes=64)
-                scale_bytes = codes_pool.tile([P, PASSES, PIXELS], U8, tag="scales", align_bytes=64)
+                words = codes_pool.tile([P, HALVES, PASSES, N_TILE], U32, tag="codes", align_bytes=64)
+                scale_bytes = codes_pool.tile([P, HALVES, PASSES, N_TILE], U8, tag="scales", align_bytes=64)
                 codes[s] = words
                 code_scales[s] = scale_bytes
-            pixels = slice(half * N_TILE, (half + 1) * N_TILE)
             nc.vector.quantize_mx(
-                out=codes[s][:, g, pixels].bitcast(FP8X4),
-                scales=code_scales[s][:, g, pixels],
-                in_=staged[s, g, half][:].rearrange("p w j -> p (w j)"),
+                out=codes[s][:, half, :, :].rearrange("p g n -> p (g n)").bitcast(FP8X4),
+                scales=code_scales[s][:, half, :, :].rearrange("p g n -> p (g n)"),
+                in_=staged[s, half][:].rearrange("p g w j -> p (g w j)"),
             )
 
         def multiply(s, unit, b):
             m, half = unit
-            pixels = slice(half * N_TILE, (half + 1) * N_TILE)
             y = bank_tile(b, [P, N_TILE], F32)
             for g in range(PASSES):
                 nc.tensor.matmul_mx(
                     out=y[:],
                     lhsT=w_words[:, g, 2 * P * m : 2 * P * (m + 1)].bitcast(FP4X4),
                     lhsT_scale=w_scales[:, g, P * m : P * (m + 1)],
-                    rhs=codes[s][:, g, pixels].bitcast(FP8X4),
-                    rhs_scale=code_scales[s][:, g, pixels],
+                    rhs=codes[s][:, half, g, :].bitcast(FP8X4),
+                    rhs_scale=code_scales[s][:, half, g, :],
                     start=(g == 0),
                     stop=(g == PASSES - 1),
                 )
@@ -284,42 +287,38 @@ def tile_axialshift_pa_t_kernel(tc, x, w1_words, w1_scales, b1, g1, be1, out):
                     if fillers:
                         fillers.pop(0)()
 
-            means = triples[s][:].rearrange("p u (e k) -> p (u e) k", k=3)[:, :, 1]
-            nc.vector.tensor_tensor(out=means, in0=means, in1=bias_per_triple[:], op=ALU.add)
+            shifted = triples[s][:].rearrange("p u (e k) -> p (u e) k", k=3)[:, :, 1:3]
+            nc.vector.tensor_tensor(out=shifted, in0=shifted, in1=shift_per_triple[:], op=ALU.add)
             fill(1)
             moments = small_pool.tile([P, 2], F32, tag="moments")
             nc.vector.bn_aggr(out=moments[:], in_=triples[s][:].rearrange("p u k -> p (u k)"))
-            fill(1)
             nc.vector.tensor_scalar(
                 out=moments[:, 1:2], in0=moments[:, 0:1], scalar1=moments[:, 0:1], scalar2=moments[:, 1:2],
                 op0=ALU.mult, op1=ALU.add,
             )
-            sample = bank_tile(M_TILES, [P, 2], F32)
-            nc.tensor.matmul(out=sample[:], lhsT=average[:], rhs=moments[:], start=True, stop=True)
+            sample = bank_tile(M_TILES, [P, 3], F32)
+            nc.tensor.matmul(out=sample[:, 0:2], lhsT=average[:], rhs=moments[:], start=True, stop=True)
+            nc.tensor.matmul(out=sample[:, 2:3], lhsT=minus_average[:], rhs=moments[:, 0:1], start=True, stop=True)
             fill(1)
             mean = sample[:, 0:1]
             mean_of_squares = sample[:, 1:2]
-            work = small_pool.tile([P, 3], F32, tag="work")
+            work = small_pool.tile([P, 2], F32, tag="work")
             nc.vector.tensor_scalar(
-                out=work[:, 0:1], in0=mean, scalar1=mean, scalar2=mean_of_squares, op0=ALU.mult, op1=ALU.subtract
+                out=work[:, 0:1], in0=mean, scalar1=sample[:, 2:3], scalar2=mean_of_squares, op0=ALU.mult, op1=ALU.add
             )
             nc.vector.scalar_tensor_tensor(
                 out=factors[:, M_TILES:], in0=bias, scalar=mean, in1=gamma, op0=ALU.subtract, op1=ALU.mult
             )
-            nc.gpsimd.tensor_scalar(
-                out=work[:, 1:2], in0=work[:, 0:1], scalar1=-1.0, scalar2=EPS, op0=ALU.mult, op1=ALU.add
-            )
-            nc.gpsimd.tensor_tensor(out=work[:, 2:3], in0=work[:, 1:2], in1=minus_half[:], op=ALU.pow)
-            fill(1)
+            nc.gpsimd.tensor_tensor(out=work[:, 1:2], in0=work[:, 0:1], in1=minus_half[:], op=ALU.pow)
             pair = small_pool.tile([P, 2 * M_TILES], F32, tag="pair")
             nc.vector.scalar_tensor_tensor(
-                out=pair[:], in0=factors[:], scalar=work[:, 2:3], in1=addends[:], op0=ALU.mult, op1=ALU.add
+                out=pair[:], in0=factors[:], scalar=work[:, 1:2], in1=addends[:], op0=ALU.mult, op1=ALU.add
             )
             coefficients[s] = pair
             fill(len(fillers))
 
-        def quantiser(s, g, half):
-            return lambda: quantise_block(s, g, half)
+        def quantiser(s, half):
+            return lambda: quantise_half(s, half)
 
         def regrouper(s, g, half):
             return lambda: regroup_part(s, g, half, "V")
@@ -327,8 +326,8 @@ def tile_axialshift_pa_t_kernel(tc, x, w1_words, w1_scales, b1, g1, be1, out):
         def vector_work(k):
             calls = []
             if exists(k + 1):
-                calls += [regrouper(k + 1, g, 0) for g in range(PASSES)]
-                calls += [quantiser(k + 1, g, 0) for g in range(PASSES)]
+                calls += [regrouper(k + 1, g, 0) for g in range(PASSES) if parts_of(k + 1, g, 0, "V")]
+                calls += [quantiser(k + 1, 0)]
             return calls
 
         load_sample(0, split=True)
@@ -341,8 +340,7 @@ def tile_axialshift_pa_t_kernel(tc, x, w1_words, w1_scales, b1, g1, be1, out):
                 regroup_part(0, g, half, "V")
                 regroup_part(0, g, half, "S")
             if half == 0:
-                for g in range(PASSES):
-                    quantise_block(0, g, half)
+                quantise_half(0, half)
                 for m in FIRST_ORDER:
                     multiply(0, (m, 0), M_TILES + m)
         for g in range(PASSES):
@@ -351,8 +349,7 @@ def tile_axialshift_pa_t_kernel(tc, x, w1_words, w1_scales, b1, g1, be1, out):
         for k in range(SAMPLES + 1):
             load_sample(k + LOADS_AHEAD, split=False)
             if exists(k):
-                for g in reversed(range(PASSES)):
-                    quantise_block(k, g, 1)
+                quantise_half(k, 1)
             regroup(k + 1, "G")
             if k == SAMPLES:
                 for m in range(M_TILES):

@@ -40,8 +40,8 @@ FIRST_PLAN = {
     (0, 1): [("V", 256), ("S", 256)], (1, 1): [("V", 256), ("S", 256)],
 }
 PLAN = {
-    (0, 0): [("S", 512)], (1, 0): [("V", 192), ("S", 320)],
-    (0, 1): [("G", 416), ("S", 96)], (1, 1): [("G", 416), ("S", 96)],
+    (0, 0): [("S", 512)], (1, 0): [("S", 512)],
+    (0, 1): [("G", 512)], (1, 1): [("G", 320), ("V", 192)],
 }
 
 FLOPS = 2 * SAMPLES * CHANNELS_OUT * CHANNELS_IN * PIXELS
@@ -326,7 +326,12 @@ def tile_axialshift_pa_t_kernel(tc, x, w1_words, w1_scales, b1, g1, be1, out):
         def vector_work(k):
             calls = []
             if exists(k + 1):
-                calls += [regrouper(k + 1, g, 0) for g in range(PASSES) if parts_of(k + 1, g, 0, "V")]
+                calls += [
+                    regrouper(k + 1, g, half)
+                    for half in range(HALVES)
+                    for g in range(PASSES)
+                    if parts_of(k + 1, g, half, "V")
+                ]
                 calls += [quantiser(k + 1, 0)]
             return calls
 

@@ -230,16 +230,26 @@ def tile_axialshift_pa_t_kernel(tc, x, w1_words, w1_scales, b1, g1, be1, out):
                     in_=turned[s, g, half][:],
                 )
 
+        def code_tiles(s):
+            words = codes_pool.tile([P, HALVES, PASSES, N_TILE], U32, tag="codes", align_bytes=64)
+            scale_bytes = codes_pool.tile([P, HALVES, PASSES, N_TILE], U8, tag="scales", align_bytes=64)
+            codes[s] = words
+            code_scales[s] = scale_bytes
+
         def quantise_half(s, half):
             if s not in codes:
-                words = codes_pool.tile([P, HALVES, PASSES, N_TILE], U32, tag="codes", align_bytes=64)
-                scale_bytes = codes_pool.tile([P, HALVES, PASSES, N_TILE], U8, tag="scales", align_bytes=64)
-                codes[s] = words
-                code_scales[s] = scale_bytes
+                code_tiles(s)
             nc.vector.quantize_mx(
                 out=codes[s][:, half, :, :].rearrange("p g n -> p (g n)").bitcast(FP8X4),
                 scales=code_scales[s][:, half, :, :].rearrange("p g n -> p (g n)"),
                 in_=staged[s, half][:].rearrange("p g w j -> p (g w j)"),
+            )
+
+        def quantise_block(s, g, half):
+            nc.vector.quantize_mx(
+                out=codes[s][:, half, g, :].bitcast(FP8X4),
+                scales=code_scales[s][:, half, g, :],
+                in_=staged[s, half][:, g, :, :].rearrange("p w j -> p (w j)"),
             )
 
         def multiply(s, unit, b):
@@ -278,7 +288,10 @@ def tile_axialshift_pa_t_kernel(tc, x, w1_words, w1_scales, b1, g1, be1, out):
                 scale=coefficients[s][:, m : m + 1],
             )
             results[s, m][1] += 1
-            if results[s, m][1] == HALVES:
+            if s == SAMPLES - 1:
+                cols = slice(half * N_TILE, (half + 1) * N_TILE)
+                nc.sync.dma_start(out=out_tiles[s, m][:, cols], in_=results[s, m][0][:, cols])
+            elif results[s, m][1] == HALVES:
                 nc.sync.dma_start(out=out_tiles[s, m], in_=results[s, m][0][:])
 
         def chain(s, fillers):
@@ -345,7 +358,9 @@ def tile_axialshift_pa_t_kernel(tc, x, w1_words, w1_scales, b1, g1, be1, out):
                 regroup_part(0, g, half, "V")
                 regroup_part(0, g, half, "S")
             if half == 0:
-                quantise_half(0, half)
+                code_tiles(0)
+                for g in range(PASSES):
+                    quantise_block(0, g, half)
                 for m in FIRST_ORDER:
                     multiply(0, (m, 0), M_TILES + m)
         for g in range(PASSES):
@@ -353,7 +368,10 @@ def tile_axialshift_pa_t_kernel(tc, x, w1_words, w1_scales, b1, g1, be1, out):
 
         for k in range(SAMPLES + 1):
             load_sample(k + LOADS_AHEAD, split=False)
-            if exists(k):
+            if k == 0:
+                for g in range(PASSES):
+                    quantise_block(0, g, 1)
+            elif exists(k):
                 quantise_half(k, 1)
             regroup(k + 1, "G")
             if k == SAMPLES:

@@ -40,7 +40,7 @@ FIRST_PLAN = {
     (0, 1): [("V", 256), ("S", 256)], (1, 1): [("V", 256), ("S", 256)],
 }
 PLAN = {
-    (0, 0): [("S", 512)], (1, 0): [("S", 512)],
+    (0, 0): [("S", 512)], (1, 0): [("S", 384), ("V", 128)],
     (0, 1): [("G", 512)], (1, 1): [("G", 320), ("V", 192)],
 }
 
@@ -86,6 +86,8 @@ def tile_axialshift_pa_t_kernel(tc, x, w1_words, w1_scales, b1, g1, be1, out):
         nc.vector.memset(average[:], 1.0 / P)
         minus_average = consts.tile([P, P], F32)
         nc.vector.memset(minus_average[:], -1.0 / P)
+        identity_f32 = consts.tile([P, P], F32)
+        make_identity(nc, identity_f32[:])
         minus_half = consts.tile([P, 1], F32)
         nc.vector.memset(minus_half[:], -0.5)
         per_channel = consts.tile([P, 3 * M_TILES], F32)
@@ -294,25 +296,36 @@ def tile_axialshift_pa_t_kernel(tc, x, w1_words, w1_scales, b1, g1, be1, out):
             elif results[s, m][1] == HALVES:
                 nc.sync.dma_start(out=out_tiles[s, m], in_=results[s, m][0][:])
 
-        def chain(s, fillers):
-            def fill(n):
-                for i in range(n):
-                    if fillers:
-                        fillers.pop(0)()
-
-            shifted = triples[s][:].rearrange("p u (e k) -> p (u e) k", k=3)[:, :, 1:3]
+        def chain(k):
+            following = exists(k + 1)
+            if following:
+                for g in range(PASSES):
+                    regroup_part(k + 1, g, 1, "V")
+                if k == 0:
+                    for g in range(PASSES):
+                        regroup_part(k + 1, g, 0, "V")
+            shifted = triples[k][:].rearrange("p u (e k) -> p (u e) k", k=3)[:, :, 1:3]
             nc.vector.tensor_tensor(out=shifted, in0=shifted, in1=shift_per_triple[:], op=ALU.add)
-            fill(1)
+            if following:
+                quantise_half(k + 1, 0)
+                multiply(k + 1, (FIRST_ORDER[0], 0), M_TILES + FIRST_ORDER[0])
             moments = small_pool.tile([P, 2], F32, tag="moments")
-            nc.vector.bn_aggr(out=moments[:], in_=triples[s][:].rearrange("p u k -> p (u k)"))
+            nc.vector.bn_aggr(out=moments[:], in_=triples[k][:].rearrange("p u k -> p (u k)"))
+            if exists(k + 2):
+                for g in range(PASSES):
+                    regroup_part(k + 2, g, 0, "V")
             nc.vector.tensor_scalar(
                 out=moments[:, 1:2], in0=moments[:, 0:1], scalar1=moments[:, 0:1], scalar2=moments[:, 1:2],
                 op0=ALU.mult, op1=ALU.add,
             )
-            sample = bank_tile(M_TILES, [P, 3], F32)
+            sample = bank_tile(M_TILES, [P, 3 + 2 * M_TILES], F32)
+            nc.tensor.matmul(out=sample[:, 3:], lhsT=identity_f32[:], rhs=addends[:], start=True, stop=True)
             nc.tensor.matmul(out=sample[:, 0:2], lhsT=average[:], rhs=moments[:], start=True, stop=True)
             nc.tensor.matmul(out=sample[:, 2:3], lhsT=minus_average[:], rhs=moments[:, 0:1], start=True, stop=True)
-            fill(1)
+            if following:
+                for m in FIRST_ORDER[1:-1]:
+                    multiply(k + 1, (m, 0), M_TILES + m)
+                quantise_half(k + 1, 1)
             mean = sample[:, 0:1]
             mean_of_squares = sample[:, 1:2]
             work = small_pool.tile([P, 2], F32, tag="work")
@@ -323,30 +336,15 @@ def tile_axialshift_pa_t_kernel(tc, x, w1_words, w1_scales, b1, g1, be1, out):
                 out=factors[:, M_TILES:], in0=bias, scalar=mean, in1=gamma, op0=ALU.subtract, op1=ALU.mult
             )
             nc.gpsimd.tensor_tensor(out=work[:, 1:2], in0=work[:, 0:1], in1=minus_half[:], op=ALU.pow)
+            if following:
+                statistics(k + 1, (FIRST_ORDER[0], 0))
             pair = small_pool.tile([P, 2 * M_TILES], F32, tag="pair")
             nc.vector.scalar_tensor_tensor(
-                out=pair[:], in0=factors[:], scalar=work[:, 1:2], in1=addends[:], op0=ALU.mult, op1=ALU.add
+                out=pair[:], in0=factors[:], scalar=work[:, 1:2], in1=sample[:, 3:], op0=ALU.mult, op1=ALU.add
             )
-            coefficients[s] = pair
-            fill(len(fillers))
-
-        def quantiser(s, half):
-            return lambda: quantise_half(s, half)
-
-        def regrouper(s, g, half):
-            return lambda: regroup_part(s, g, half, "V")
-
-        def vector_work(k):
-            calls = []
-            if exists(k + 1):
-                calls += [
-                    regrouper(k + 1, g, half)
-                    for half in range(HALVES)
-                    for g in range(PASSES)
-                    if parts_of(k + 1, g, half, "V")
-                ]
-                calls += [quantiser(k + 1, 0)]
-            return calls
+            coefficients[k] = pair
+            if following:
+                multiply(k + 1, (FIRST_ORDER[-1], 0), M_TILES + FIRST_ORDER[-1])
 
         load_sample(0, split=True)
         load_sample(1, split=False)
@@ -371,9 +369,7 @@ def tile_axialshift_pa_t_kernel(tc, x, w1_words, w1_scales, b1, g1, be1, out):
             if k == 0:
                 for g in range(PASSES):
                     quantise_block(0, g, 1)
-            elif exists(k):
-                quantise_half(k, 1)
-            regroup(k + 1, "G")
+                regroup(1, "G")
             if k == SAMPLES:
                 for m in range(M_TILES):
                     multiply(k - 1, (m, 0), M_TILES + m)
@@ -387,7 +383,7 @@ def tile_axialshift_pa_t_kernel(tc, x, w1_words, w1_scales, b1, g1, be1, out):
                 if exists(k):
                     multiply(k, (m, 1), m)
             if exists(k):
-                for m in FIRST_ORDER:
+                for m in FIRST_ORDER[min(k, 1):]:
                     statistics(k, (m, 0))
                 for m in range(M_TILES):
                     statistics(k, (m, 1))
@@ -405,7 +401,5 @@ def tile_axialshift_pa_t_kernel(tc, x, w1_words, w1_scales, b1, g1, be1, out):
             if k == 0:
                 spread_constants()
             if exists(k):
-                chain(k, vector_work(k))
-            if exists(k + 1):
-                for m in FIRST_ORDER:
-                    multiply(k + 1, (m, 0), M_TILES + m)
+                chain(k)
+            regroup(k + 2, "G")

@@ -40,7 +40,7 @@ FIRST_PLAN = {
     (0, 1): [("V", 256), ("S", 256)], (1, 1): [("V", 256), ("S", 256)],
 }
 PLAN = {
-    (0, 0): [("S", 512)], (1, 0): [("S", 384), ("V", 128)],
+    (0, 0): [("S", 512)], (1, 0): [("S", 512)],
     (0, 1): [("G", 512)], (1, 1): [("G", 320), ("V", 192)],
 }
 

@@ -40,15 +40,21 @@ FIRST_PLAN = {
     (0, 1): [("V", 256), ("S", 256)], (1, 1): [("V", 256), ("S", 256)],
 }
 PLAN = {
-    (0, 0): [("S", 512)], (1, 0): [("S", 512)],
-    (0, 1): [("G", 512)], (1, 1): [("G", 320), ("V", 192)],
+    (0, 0): [("S", 448), ("V", 64)], (1, 0): [("S", 448), ("V", 64)],
+    (0, 1): [("G", 416), ("V", 96)], (1, 1): [("G", 416), ("V", 96)],
 }
 
 FLOPS = 2 * SAMPLES * CHANNELS_OUT * CHANNELS_IN * PIXELS
 
 
+EARLY_PLAN = {
+    (0, 0): [("S", 512)], (1, 0): [("S", 512)],
+    (0, 1): PLAN[0, 1], (1, 1): PLAN[1, 1],
+}
+
+
 def plan_of(s):
-    return FIRST_PLAN if s == 0 else PLAN
+    return FIRST_PLAN if s == 0 else EARLY_PLAN if s == 1 else PLAN
 
 
 def tile_axialshift_pa_t_kernel(tc, x, w1_words, w1_scales, b1, g1, be1, out):
@@ -157,7 +163,7 @@ def tile_axialshift_pa_t_kernel(tc, x, w1_words, w1_scales, b1, g1, be1, out):
                     for g in range(PASSES):
                         cols = slice(half * N_TILE, (half + 1) * N_TILE)
                         nc.sync.dma_start(out=raw[s, g][:, :, cols], in_=x_chunks[s, g][:, :, cols])
-                    if half == 0:
+                    if s == 0 and half == 0:
                         load_constants()
             else:
                 for g in range(PASSES):
@@ -182,6 +188,8 @@ def tile_axialshift_pa_t_kernel(tc, x, w1_words, w1_scales, b1, g1, be1, out):
             return found
 
         def regroup_part(s, g, half, engine):
+            if not exists(s):
+                return
             for first, width in parts_of(s, g, half, engine):
                 target = stage_of(s, half)[:, g, first : first + width, :]
                 source = raw[s, g][:, :, half * N_TILE + first : half * N_TILE + first + width]
@@ -297,23 +305,13 @@ def tile_axialshift_pa_t_kernel(tc, x, w1_words, w1_scales, b1, g1, be1, out):
                 nc.sync.dma_start(out=out_tiles[s, m], in_=results[s, m][0][:])
 
         def chain(k):
-            following = exists(k + 1)
-            if following:
-                for g in range(PASSES):
-                    regroup_part(k + 1, g, 1, "V")
-                if k == 0:
-                    for g in range(PASSES):
-                        regroup_part(k + 1, g, 0, "V")
+            regroup_part(k + 1, 0, 1, "V")
             shifted = triples[k][:].rearrange("p u (e k) -> p (u e) k", k=3)[:, :, 1:3]
             nc.vector.tensor_tensor(out=shifted, in0=shifted, in1=shift_per_triple[:], op=ALU.add)
-            if following:
-                quantise_half(k + 1, 0)
-                multiply(k + 1, (FIRST_ORDER[0], 0), M_TILES + FIRST_ORDER[0])
+            regroup_part(k + 1, 1, 1, "V")
             moments = small_pool.tile([P, 2], F32, tag="moments")
             nc.vector.bn_aggr(out=moments[:], in_=triples[k][:].rearrange("p u k -> p (u k)"))
-            if exists(k + 2):
-                for g in range(PASSES):
-                    regroup_part(k + 2, g, 0, "V")
+            regroup_part(k + 2, 0, 0, "V")
             nc.vector.tensor_scalar(
                 out=moments[:, 1:2], in0=moments[:, 0:1], scalar1=moments[:, 0:1], scalar2=moments[:, 1:2],
                 op0=ALU.mult, op1=ALU.add,
@@ -322,10 +320,11 @@ def tile_axialshift_pa_t_kernel(tc, x, w1_words, w1_scales, b1, g1, be1, out):
             nc.tensor.matmul(out=sample[:, 3:], lhsT=identity_f32[:], rhs=addends[:], start=True, stop=True)
             nc.tensor.matmul(out=sample[:, 0:2], lhsT=average[:], rhs=moments[:], start=True, stop=True)
             nc.tensor.matmul(out=sample[:, 2:3], lhsT=minus_average[:], rhs=moments[:, 0:1], start=True, stop=True)
-            if following:
-                for m in FIRST_ORDER[1:-1]:
+            regroup_part(k + 2, 1, 0, "V")
+            if exists(k + 1):
+                quantise_half(k + 1, 0)
+                for m in FIRST_ORDER[:-1]:
                     multiply(k + 1, (m, 0), M_TILES + m)
-                quantise_half(k + 1, 1)
             mean = sample[:, 0:1]
             mean_of_squares = sample[:, 1:2]
             work = small_pool.tile([P, 2], F32, tag="work")
@@ -336,18 +335,19 @@ def tile_axialshift_pa_t_kernel(tc, x, w1_words, w1_scales, b1, g1, be1, out):
                 out=factors[:, M_TILES:], in0=bias, scalar=mean, in1=gamma, op0=ALU.subtract, op1=ALU.mult
             )
             nc.gpsimd.tensor_tensor(out=work[:, 1:2], in0=work[:, 0:1], in1=minus_half[:], op=ALU.pow)
-            if following:
+            if exists(k + 1):
+                quantise_half(k + 1, 1)
                 statistics(k + 1, (FIRST_ORDER[0], 0))
             pair = small_pool.tile([P, 2 * M_TILES], F32, tag="pair")
             nc.vector.scalar_tensor_tensor(
                 out=pair[:], in0=factors[:], scalar=work[:, 1:2], in1=sample[:, 3:], op0=ALU.mult, op1=ALU.add
             )
             coefficients[k] = pair
-            if following:
+            if exists(k + 1):
                 multiply(k + 1, (FIRST_ORDER[-1], 0), M_TILES + FIRST_ORDER[-1])
 
         load_sample(0, split=True)
-        load_sample(1, split=False)
+        load_sample(1, split=True)
         load_vectors()
         for s in range(2, LOADS_AHEAD):
             load_sample(s, split=False)
@@ -387,17 +387,14 @@ def tile_axialshift_pa_t_kernel(tc, x, w1_words, w1_scales, b1, g1, be1, out):
                     statistics(k, (m, 0))
                 for m in range(M_TILES):
                     statistics(k, (m, 1))
-            if exists(k + 1):
-                for g in range(PASSES):
-                    regroup_part(k + 1, g, 1, "S")
-            if exists(k + 2):
-                regroup_part(k + 2, 0, 0, "S")
+            for g in range(PASSES):
+                regroup_part(k + 1, g, 1, "S")
+            regroup_part(k + 2, 0, 0, "S")
             for m in range(M_TILES):
                 if exists(k - 1):
                     multiply(k - 1, (m, 0), M_TILES + m)
                     gelu(k - 1, (m, 0))
-            if exists(k + 2):
-                regroup_part(k + 2, 1, 0, "S")
+            regroup_part(k + 2, 1, 0, "S")
             if k == 0:
                 spread_constants()
             if exists(k):

@@ -298,7 +298,7 @@ def tile_axialshift_pa_t_kernel(tc, x, w1_words, w1_scales, b1, g1, be1, out):
                 scale=coefficients[s][:, m : m + 1],
             )
             results[s, m][1] += 1
-            if s == SAMPLES - 1:
+            if s >= SAMPLES - 2:
                 cols = slice(half * N_TILE, (half + 1) * N_TILE)
                 nc.sync.dma_start(out=out_tiles[s, m][:, cols], in_=results[s, m][0][:, cols])
             elif results[s, m][1] == HALVES:
@@ -343,6 +343,11 @@ def tile_axialshift_pa_t_kernel(tc, x, w1_words, w1_scales, b1, g1, be1, out):
                 out=pair[:], in0=factors[:], scalar=work[:, 1:2], in1=sample[:, 3:], op0=ALU.mult, op1=ALU.add
             )
             coefficients[k] = pair
+            if k == SAMPLES - 1:
+                multiply(k - 1, (M_TILES - 1, 0), 2 * M_TILES - 1)
+                gelu(k - 1, (M_TILES - 1, 0))
+                for m in FIRST_ORDER[:-1]:
+                    multiply(k, (m, 0), M_TILES + m)
             if exists(k + 1):
                 multiply(k + 1, (FIRST_ORDER[-1], 0), M_TILES + FIRST_ORDER[-1])
 
@@ -371,9 +376,8 @@ def tile_axialshift_pa_t_kernel(tc, x, w1_words, w1_scales, b1, g1, be1, out):
                     quantise_block(0, g, 1)
                 regroup(1, "G")
             if k == SAMPLES:
-                for m in range(M_TILES):
-                    multiply(k - 1, (m, 0), M_TILES + m)
-                for m in range(M_TILES):
+                multiply(k - 1, (0, 0), M_TILES)
+                for m in FIRST_ORDER:
                     gelu(k - 1, (m, 1))
                     gelu(k - 1, (m, 0))
                 break
@@ -390,7 +394,7 @@ def tile_axialshift_pa_t_kernel(tc, x, w1_words, w1_scales, b1, g1, be1, out):
             for g in range(PASSES):
                 regroup_part(k + 1, g, 1, "S")
             regroup_part(k + 2, 0, 0, "S")
-            for m in range(M_TILES):
+            for m in range(M_TILES - 1 if k == SAMPLES - 1 else M_TILES):
                 if exists(k - 1):
                     multiply(k - 1, (m, 0), M_TILES + m)
                     gelu(k - 1, (m, 0))

@@ -53,8 +53,14 @@ EARLY_PLAN = {
 }
 
 
+SECOND_PLAN = {
+    (0, 0): [("S", 512)], (1, 0): [("S", 512)],
+    (0, 1): PLAN[0, 1], (1, 1): PLAN[1, 1],
+}
+
+
 def plan_of(s):
-    return FIRST_PLAN if s == 0 else EARLY_PLAN if s == 1 else PLAN
+    return FIRST_PLAN if s == 0 else EARLY_PLAN if s == 1 else SECOND_PLAN if s == 2 else PLAN
 
 
 def tile_axialshift_pa_t_kernel(tc, x, w1_words, w1_scales, b1, g1, be1, out):
@@ -66,6 +72,7 @@ def tile_axialshift_pa_t_kernel(tc, x, w1_words, w1_scales, b1, g1, be1, out):
     with ExitStack() as ctx:
         consts = ctx.enter_context(tc.tile_pool(name="consts", bufs=1))
         raw_pool = ctx.enter_context(tc.tile_pool(name="raw", bufs=RAW_BUFS))
+        early_pool = ctx.enter_context(tc.tile_pool(name="early", bufs=8))
         stage_pool = ctx.enter_context(tc.tile_pool(name="stage", bufs=1))
         codes_pool = ctx.enter_context(tc.tile_pool(name="codes", bufs=3))
         small_pool = ctx.enter_context(tc.tile_pool(name="small", bufs=3))
@@ -155,19 +162,21 @@ def tile_axialshift_pa_t_kernel(tc, x, w1_words, w1_scales, b1, g1, be1, out):
         def load_sample(s, split):
             if not exists(s):
                 return
-            for g in range(PASSES):
-                chunk = raw_pool.tile([P, PACK, PIXELS], BF16, tag="raw")
-                raw[s, g] = chunk
             if split:
                 for half in range(HALVES):
+                    cols = slice(half * N_TILE, (half + 1) * N_TILE)
                     for g in range(PASSES):
-                        cols = slice(half * N_TILE, (half + 1) * N_TILE)
-                        nc.sync.dma_start(out=raw[s, g][:, :, cols], in_=x_chunks[s, g][:, :, cols])
+                        piece = early_pool.tile([P, PACK, N_TILE], BF16, tag="piece")
+                        nc.sync.dma_start(out=piece[:], in_=x_chunks[s, g][:, :, cols])
+                        raw[s, g, half] = piece[:]
                     if s == 0 and half == 0:
                         load_constants()
             else:
                 for g in range(PASSES):
-                    nc.sync.dma_start(out=raw[s, g][:], in_=x_chunks[s, g])
+                    chunk = raw_pool.tile([P, PACK, PIXELS], BF16, tag="raw")
+                    nc.sync.dma_start(out=chunk[:], in_=x_chunks[s, g])
+                    for half in range(HALVES):
+                        raw[s, g, half] = chunk[:, :, half * N_TILE : (half + 1) * N_TILE]
 
         def stage_of(s, half):
             if (s, half) not in staged:
@@ -192,7 +201,7 @@ def tile_axialshift_pa_t_kernel(tc, x, w1_words, w1_scales, b1, g1, be1, out):
                 return
             for first, width in parts_of(s, g, half, engine):
                 target = stage_of(s, half)[:, g, first : first + width, :]
-                source = raw[s, g][:, :, half * N_TILE + first : half * N_TILE + first + width]
+                source = raw[s, g, half][:, :, first : first + width]
                 if engine == "V":
                     nc.vector.tensor_copy(
                         out=target.rearrange("p (c i) j -> p c j i", i=RUN),
@@ -216,29 +225,6 @@ def tile_axialshift_pa_t_kernel(tc, x, w1_words, w1_scales, b1, g1, be1, out):
             for half in range(HALVES):
                 for g in range(PASSES):
                     regroup_part(s, g, half, engine)
-
-        turned = {}
-
-        def turn(s, g, half, b):
-            for first, width in parts_of(s, g, half, "T"):
-                bank = bank_tile(b, [P, width * PACK], BF16)
-                for c in range(0, width, N_TILE // PACK):
-                    cols = slice(half * N_TILE + first + c, half * N_TILE + first + c + N_TILE // PACK)
-                    nc.tensor.matmul(
-                        out=bank[:, c * PACK : c * PACK + N_TILE],
-                        lhsT=identity[:],
-                        rhs=raw[s, g][:, :, cols].rearrange("p j w -> p w j"),
-                        start=True,
-                        stop=True,
-                    )
-                turned[s, g, half] = bank
-
-        def fetch(s, g, half):
-            for first, width in parts_of(s, g, half, "T"):
-                nc.scalar.copy(
-                    out=stage_of(s, g, half)[:, first : first + width, :].rearrange("p w j -> p (w j)"),
-                    in_=turned[s, g, half][:],
-                )
 
         def code_tiles(s):
             words = codes_pool.tile([P, HALVES, PASSES, N_TILE], U32, tag="codes", align_bytes=64)

from contextlib import ExitStack

import concourse.mybir as mybir
from concourse.masks import make_identity

F32 = mybir.dt.float32
BF16 = mybir.dt.bfloat16
I32 = mybir.dt.int32
U8 = mybir.dt.uint8
U32 = mybir.dt.uint32
FP8X4 = mybir.dt.float8_e4m3fn_x4
FP4X4 = mybir.dt.float4_e2m1fn_x4
ALU = mybir.AluOpType
ACT = mybir.ActivationFunctionType

P = 128
PACK = 4
SAMPLES = 8
CHANNELS_IN = 1024
CHANNELS_OUT = 512
PIXELS = 1024
EPS = 1e-5

PASSES = CHANNELS_IN // (P * PACK)
M_TILES = CHANNELS_OUT // P
N_TILE = 512
HALVES = PIXELS // N_TILE
UNITS = M_TILES * HALVES
BANKS = 8
RUN = 4


FIRST_ORDER = (1, 2, 3, 0)

LOADS_AHEAD = 4
RAW_BUFS = 2 * LOADS_AHEAD

FIRST_PLAN = {
    (0, 0): [("V", 256), ("S", 256)], (1, 0): [("V", 256), ("S", 256)],
    (0, 1): [("V", 256), ("S", 256)], (1, 1): [("V", 256), ("S", 256)],
}
PLAN = {
    (0, 0): [("S", 448), ("V", 64)], (1, 0): [("S", 448), ("V", 64)],
    (0, 1): [("G", 416), ("V", 96)], (1, 1): [("G", 416), ("V", 96)],
}

FLOPS = 2 * SAMPLES * CHANNELS_OUT * CHANNELS_IN * PIXELS


EARLY_PLAN = {
    (0, 0): [("S", 512)], (1, 0): [("S", 512)],
    (0, 1): PLAN[0, 1], (1, 1): PLAN[1, 1],
}


SECOND_PLAN = {
    (0, 0): [("S", 512)], (1, 0): [("S", 512)],
    (0, 1): PLAN[0, 1], (1, 1): PLAN[1, 1],
}


def plan_of(s):
    return FIRST_PLAN if s == 0 else EARLY_PLAN if s == 1 else SECOND_PLAN if s == 2 else PLAN


def tile_axialshift_pa_t_kernel(tc, x, w1_words, w1_scales, b1, g1, be1, out):
    nc = tc.nc

    x_chunks = x.rearrange("s (g p j) h w -> s g p j (h w)", g=PASSES, p=P, j=PACK)
    out_tiles = out.rearrange("s (m p) h w -> s m p (h w)", p=P)

    with ExitStack() as ctx:
        consts = ctx.enter_context(tc.tile_pool(name="consts", bufs=1))
        raw_pool = ctx.enter_context(tc.tile_pool(name="raw", bufs=RAW_BUFS))
        early_pool = ctx.enter_context(tc.tile_pool(name="early", bufs=8))
        stage_pool = ctx.enter_context(tc.tile_pool(name="stage", bufs=1))
        codes_pool = ctx.enter_context(tc.tile_pool(name="codes", bufs=3))
        small_pool = ctx.enter_context(tc.tile_pool(name="small", bufs=3))
        result_pool = ctx.enter_context(tc.tile_pool(name="result", bufs=8))
        psum = ctx.enter_context(tc.psum_pool(name="psum", bufs=1))
        ctx.enter_context(tc.manual_schedule())

        def bank_tile(b, shape, dtype):
            bank = psum.tile(shape, dtype, tag="bank%d" % b, name="bank%d" % b)
            return bank

        warm = consts.tile([P, 1], F32)
        nc.vector.memset(warm[:], 0.0)
        nc.scalar.activation(out=warm[:], in_=warm[:], func=ACT.Gelu)

        w_words = consts.tile([P, PASSES, 2 * CHANNELS_OUT], U8, align_bytes=64)
        w_scales = consts.tile([P, PASSES, CHANNELS_OUT], U8, align_bytes=64)
        nc.vector.memset(w_scales[:].bitcast(I32), 0)
        identity = consts.tile([P, P], BF16)
        make_identity(nc, identity[:])
        vector_rows = consts.tile([P, P], BF16)
        nc.vector.memset(vector_rows[:], 0.0)
        average = consts.tile([P, P], F32)
        nc.vector.memset(average[:], 1.0 / P)
        minus_average = consts.tile([P, P], F32)
        nc.vector.memset(minus_average[:], -1.0 / P)
        identity_f32 = consts.tile([P, P], F32)
        make_identity(nc, identity_f32[:])
        minus_half = consts.tile([P, 1], F32)
        nc.vector.memset(minus_half[:], -0.5)
        per_channel = consts.tile([P, 3 * M_TILES], F32)
        bias = per_channel[:, 0:M_TILES]
        gamma = per_channel[:, M_TILES : 2 * M_TILES]
        shift_per_triple = consts.tile([P, 2 * UNITS, 2], F32)
        nc.vector.memset(shift_per_triple[:], 0.0)
        nc.vector.tensor_scalar(
            out=shift_per_triple[:, :, 1], in0=shift_per_triple[:, :, 1], scalar1=EPS * N_TILE / 2, scalar2=None,
            op0=ALU.add,
        )
        factors = consts.tile([P, 2 * M_TILES], F32)
        addends = consts.tile([P, 2 * M_TILES], F32)
        nc.vector.memset(addends[:], 0.0)

        def load_constants():
            nc.sync.dma_start(
                out=w_words[:].bitcast(I32), in_=w1_words.rearrange("g p n -> p g n").bitcast(I32)
            )
            for quadrant in range(4):
                nc.sync.dma_start(
                    out=w_scales[32 * quadrant : 32 * quadrant + 4, :, :].bitcast(I32),
                    in_=w1_scales[:, 4 * quadrant : 4 * quadrant + 4, :]
                    .rearrange("g r n -> r g n")
                    .bitcast(I32),
                )

        def load_vectors():
            for i, vector in enumerate((b1, g1, be1)):
                nc.sync.dma_start(
                    out=vector_rows[M_TILES * i : M_TILES * (i + 1), :],
                    in_=vector.rearrange("(m p) -> m p", p=P),
                )

        def spread_constants():
            vector_columns = bank_tile(M_TILES + 1, [P, P], BF16)
            nc.tensor.transpose(vector_columns[:], vector_rows[:], identity[:])
            nc.vector.tensor_copy(out=per_channel[:], in_=vector_columns[:, 0 : 3 * M_TILES])
            nc.vector.tensor_copy(
                out=shift_per_triple[:, :, 0].rearrange("p (m r) -> p m r", m=M_TILES),
                in_=bias.unsqueeze(2).to_broadcast([P, M_TILES, 2 * HALVES]),
            )
            nc.vector.tensor_copy(out=factors[:, 0:M_TILES], in_=gamma)
            nc.vector.tensor_copy(out=addends[:, M_TILES:], in_=per_channel[:, 2 * M_TILES : 3 * M_TILES])

        raw = {}
        staged = {}
        codes = {}
        code_scales = {}
        triples = {}
        coefficients = {}
        results = {}
        bank_of = {}
        y_tiles = {}

        def exists(s):
            return 0 <= s < SAMPLES

        def load_sample(s, split):
            if not exists(s):
                return
            if split:
                for half in range(HALVES):
                    cols = slice(half * N_TILE, (half + 1) * N_TILE)
                    for g in range(PASSES):
                        piece = early_pool.tile([P, PACK, N_TILE], BF16, tag="piece")
                        nc.sync.dma_start(out=piece[:], in_=x_chunks[s, g][:, :, cols])
                        raw[s, g, half] = piece[:]
                    if s == 0 and half == 0:
                        load_constants()
            else:
                for g in range(PASSES):
                    chunk = raw_pool.tile([P, PACK, PIXELS], BF16, tag="raw")
                    nc.sync.dma_start(out=chunk[:], in_=x_chunks[s, g])
                    for half in range(HALVES):
                        raw[s, g, half] = chunk[:, :, half * N_TILE : (half + 1) * N_TILE]

        def stage_of(s, half):
            if (s, half) not in staged:
                if half == 0:
                    stage = stage_pool.tile([P, PASSES, N_TILE, PACK], BF16, tag="first", bufs=3, align_bytes=64)
                else:
                    stage = stage_pool.tile([P, PASSES, N_TILE, PACK], BF16, tag="second", bufs=1, align_bytes=64)
                staged[s, half] = stage
            return staged[s, half]

        def parts_of(s, g, half, engine):
            first = 0
            found = []
            for who, width in plan_of(s)[g, half]:
                if who == engine:
                    found.append((first, width))
                first += width
            return found

        def regroup_part(s, g, half, engine):
            if not exists(s):
                return
            for first, width in parts_of(s, g, half, engine):
                target = stage_of(s, half)[:, g, first : first + width, :]
                source = raw[s, g, half][:, :, first : first + width]
                if engine == "V":
                    nc.vector.tensor_copy(
                        out=target.rearrange("p (c i) j -> p c j i", i=RUN),
                        in_=source.rearrange("p j (c i) -> p c j i", i=RUN),
                    )
                elif engine == "S":
                    nc.scalar.copy(out=target, in_=source.rearrange("p j w -> p w j"))
                else:
                    nc.gpsimd.tensor_scalar(
                        out=target,
                        in0=source.rearrange("p j w -> p w j"),
                        scalar1=1.0,
                        scalar2=0.0,
                        op0=ALU.mult,
                        op1=ALU.add,
                    )

        def regroup(s, engine):
            if not exists(s):
                return
            for half in range(HALVES):
                for g in range(PASSES):
                    regroup_part(s, g, half, engine)

        def code_tiles(s):
            words = codes_pool.tile([P, HALVES, PASSES, N_TILE], U32, tag="codes", align_bytes=64)
            scale_bytes = codes_pool.tile([P, HALVES, PASSES, N_TILE], U8, tag="scales", align_bytes=64)
            codes[s] = words
            code_scales[s] = scale_bytes

        def quantise_half(s, half):
            if s not in codes:
                code_tiles(s)
            nc.vector.quantize_mx(
                out=codes[s][:, half, :, :].rearrange("p g n -> p (g n)").bitcast(FP8X4),
                scales=code_scales[s][:, half, :, :].rearrange("p g n -> p (g n)"),
                in_=staged[s, half][:].rearrange("p g w j -> p (g w j)"),
            )

        def quantise_block(s, g, half):
            nc.vector.quantize_mx(
                out=codes[s][:, half, g, :].bitcast(FP8X4),
                scales=code_scales[s][:, half, g, :],
                in_=staged[s, half][:, g, :, :].rearrange("p w j -> p (w j)"),
            )

        def multiply(s, unit, b):
            m, half = unit
            y = bank_tile(b, [P, N_TILE], F32)
            for g in range(PASSES):
                nc.tensor.matmul_mx(
                    out=y[:],
                    lhsT=w_words[:, g, 2 * P * m : 2 * P * (m + 1)].bitcast(FP4X4),
                    lhsT_scale=w_scales[:, g, P * m : P * (m + 1)],
                    rhs=codes[s][:, half, g, :].bitcast(FP8X4),
                    rhs_scale=code_scales[s][:, half, g, :],
                    start=(g == 0),
                    stop=(g == PASSES - 1),
                )
            y_tiles[s, unit] = y
            bank_of[s, unit] = b

        def statistics(s, unit):
            if s not in triples:
                sample_triples = small_pool.tile([P, UNITS, 6], F32, tag="triples")
                triples[s] = sample_triples
            m, half = unit
            nc.vector.bn_stats(out=triples[s][:, HALVES * m + half, :], in_=y_tiles[s, unit][:])

        def gelu(s, unit):
            m, half = unit
            if (s, m) not in results:
                result = result_pool.tile([P, PIXELS], F32, tag="result")
                results[s, m] = [result, 0]
            nc.scalar.activation(
                out=results[s, m][0][:, half * N_TILE : (half + 1) * N_TILE],
                in_=y_tiles[s, unit][:],
                func=ACT.Gelu,
                bias=coefficients[s][:, M_TILES + m : M_TILES + m + 1],
                scale=coefficients[s][:, m : m + 1],
            )
            results[s, m][1] += 1
            if s >= SAMPLES - 2:
                cols = slice(half * N_TILE, (half + 1) * N_TILE)
                nc.sync.dma_start(out=out_tiles[s, m][:, cols], in_=results[s, m][0][:, cols])
            elif results[s, m][1] == HALVES:
                nc.sync.dma_start(out=out_tiles[s, m], in_=results[s, m][0][:])

        def chain(k):
            regroup_part(k + 1, 0, 1, "V")
            shifted = triples[k][:].rearrange("p u (e k) -> p (u e) k", k=3)[:, :, 1:3]
            nc.vector.tensor_tensor(out=shifted, in0=shifted, in1=shift_per_triple[:], op=ALU.add)
            regroup_part(k + 1, 1, 1, "V")
            moments = small_pool.tile([P, 2], F32, tag="moments")
            nc.vector.bn_aggr(out=moments[:], in_=triples[k][:].rearrange("p u k -> p (u k)"))
            regroup_part(k + 2, 0, 0, "V")
            nc.vector.tensor_scalar(
                out=moments[:, 1:2], in0=moments[:, 0:1], scalar1=moments[:, 0:1], scalar2=moments[:, 1:2],
                op0=ALU.mult, op1=ALU.add,
            )
            sample = bank_tile(M_TILES, [P, 3 + 2 * M_TILES], F32)
            nc.tensor.matmul(out=sample[:, 3:], lhsT=identity_f32[:], rhs=addends[:], start=True, stop=True)
            nc.tensor.matmul(out=sample[:, 0:2], lhsT=average[:], rhs=moments[:], start=True, stop=True)
            nc.tensor.matmul(out=sample[:, 2:3], lhsT=minus_average[:], rhs=moments[:, 0:1], start=True, stop=True)
            regroup_part(k + 2, 1, 0, "V")
            if exists(k + 1):
                quantise_half(k + 1, 0)
                for m in FIRST_ORDER[:-1]:
                    multiply(k + 1, (m, 0), M_TILES + m)
            mean = sample[:, 0:1]
            mean_of_squares = sample[:, 1:2]
            work = small_pool.tile([P, 2], F32, tag="work")
            nc.vector.tensor_scalar(
                out=work[:, 0:1], in0=mean, scalar1=sample[:, 2:3], scalar2=mean_of_squares, op0=ALU.mult, op1=ALU.add
            )
            nc.vector.scalar_tensor_tensor(
                out=factors[:, M_TILES:], in0=bias, scalar=mean, in1=gamma, op0=ALU.subtract, op1=ALU.mult
            )
            nc.gpsimd.tensor_tensor(out=work[:, 1:2], in0=work[:, 0:1], in1=minus_half[:], op=ALU.pow)
            if exists(k + 1):
                quantise_half(k + 1, 1)
                statistics(k + 1, (FIRST_ORDER[0], 0))
            pair = small_pool.tile([P, 2 * M_TILES], F32, tag="pair")
            nc.vector.scalar_tensor_tensor(
                out=pair[:], in0=factors[:], scalar=work[:, 1:2], in1=sample[:, 3:], op0=ALU.mult, op1=ALU.add
            )
            coefficients[k] = pair
            if k == SAMPLES - 1:
                multiply(k - 1, (M_TILES - 1, 0), 2 * M_TILES - 1)
                gelu(k - 1, (M_TILES - 1, 0))
                for m in FIRST_ORDER[:-1]:
                    multiply(k, (m, 0), M_TILES + m)
            if exists(k + 1):
                multiply(k + 1, (FIRST_ORDER[-1], 0), M_TILES + FIRST_ORDER[-1])

        load_sample(0, split=True)
        load_sample(1, split=True)
        load_vectors()
        for s in range(2, LOADS_AHEAD):
            load_sample(s, split=False)
        for half in range(HALVES):
            for g in range(PASSES):
                regroup_part(0, g, half, "V")
                regroup_part(0, g, half, "S")
            if half == 0:
                code_tiles(0)
                for g in range(PASSES):
                    quantise_block(0, g, half)
                for m in FIRST_ORDER:
                    multiply(0, (m, 0), M_TILES + m)
        for g in range(PASSES):
            regroup_part(1, g, 0, "S")

        for k in range(SAMPLES + 1):
            load_sample(k + LOADS_AHEAD, split=False)
            if k == 0:
                for g in range(PASSES):
                    quantise_block(0, g, 1)
                regroup(1, "G")
            if k == SAMPLES:
                multiply(k - 1, (0, 0), M_TILES)
                for m in FIRST_ORDER:
                    gelu(k - 1, (m, 1))
                    gelu(k - 1, (m, 0))
                break
            for m in range(M_TILES):
                if exists(k - 1):
                    gelu(k - 1, (m, 1))
                if exists(k):
                    multiply(k, (m, 1), m)
            if exists(k):
                for m in FIRST_ORDER[min(k, 1):]:
                    statistics(k, (m, 0))
                for m in range(M_TILES):
                    statistics(k, (m, 1))
            for g in range(PASSES):
                regroup_part(k + 1, g, 1, "S")
            regroup_part(k + 2, 0, 0, "S")
            for m in range(M_TILES - 1 if k == SAMPLES - 1 else M_TILES):
                if exists(k - 1):
                    multiply(k - 1, (m, 0), M_TILES + m)
                    gelu(k - 1, (m, 0))
            regroup_part(k + 2, 1, 0, "S")
            if k == 0:
                spread_constants()
            if exists(k):
                chain(k)
            regroup(k + 2, "G")
